import numpy as np
import ml_dtypes


def mxq(x, axis, fmt="e4m3"):
    dtype, down = {"e4m3": (ml_dtypes.float8_e4m3fn, 7), "e5m2": (ml_dtypes.float8_e5m2, 14)}[fmt]
    v = np.moveaxis(np.asarray(x, np.float32).astype(ml_dtypes.bfloat16).astype(np.float64), axis, -1)
    blocks = v.reshape(v.shape[:-1] + (-1, 32))
    amax = np.abs(blocks).max(-1, keepdims=True)
    byte = np.maximum(np.where(amax > 0, np.frexp(amax)[1] - 1 + 127, 0) - down, 1)
    scale = np.exp2(byte - 127.0)
    codes = (blocks / scale).astype(np.float32).astype(dtype).astype(np.float64)
    return np.moveaxis((codes * scale).reshape(v.shape), -1, axis)


WIDE = False


def mx_kscale(k):
    if not WIDE:
        return np.ones(k)
    levels = np.array([10, -10, 5, -5, 0])
    a = np.random.permutation(np.resize(levels, k // 512 * 4)).reshape(k // 512, 4)
    idx = np.arange(k)
    return np.exp2(a[idx // 512, idx % 128 // 32])


BF16 = ml_dtypes.bfloat16


def bf(x):
    return np.asarray(x, np.float32).astype(BF16)


def f64(x):
    return np.asarray(x).astype(np.float64)


E2M1 = np.array([0.0, 0.5, 1.0, 1.5, 2.0, 3.0, 4.0, 6.0, -0.0, -0.5, -1.0, -1.5, -2.0, -3.0, -4.0, -6.0])


def pack_weight(w, fmt):
    k, n = w.shape
    w = f64(bf(w)).reshape(k // 32, 32, n)
    amax = np.abs(w).max(1)
    if fmt == "e4m3":
        byte = np.frexp(amax)[1] - 1 + 127 - 7
    else:
        mant, ex = np.frexp(amax / 6.0)
        byte = np.where(mant > 0.5, ex, ex - 1) + 127
    byte = np.clip(np.where(amax > 0, byte, 1), 1, 254)
    scaled = (w * np.exp2(127.0 - byte)[:, None, :]).reshape(k, n).astype(np.float32)
    by_word = np.ascontiguousarray(scaled.reshape(k // 512, 128, 4, n).transpose(0, 1, 3, 2))
    if fmt == "e4m3":
        words = by_word.astype(ml_dtypes.float8_e4m3fn).view(np.uint8)
    else:
        c = by_word.astype(ml_dtypes.float4_e2m1fn).view(np.uint8) & 0xF
        words = c[..., 0::2] | (c[..., 1::2] << 4)
    return np.ascontiguousarray(words), np.ascontiguousarray(byte.astype(np.uint8).reshape(k // 512, 16, n))


def unpack_weight(words, scales, fmt):
    g, p, n, _ = words.shape
    if fmt == "e4m3":
        vals = np.ascontiguousarray(words).view(ml_dtypes.float8_e4m3fn).astype(np.float64)
    else:
        nib = np.empty((g, p, n, 4), np.uint8)
        nib[..., 0::2] = words & 0xF
        nib[..., 1::2] = words >> 4
        vals = E2M1[nib]
    vals = vals * np.repeat(np.exp2(scales.astype(np.float64) - 127.0), 8, axis=1)[..., None]
    return vals.transpose(0, 1, 3, 2).reshape(g * 512, n)

def pack4(w):
    words, scales = pack_weight(w, "e2m1")
    return words.reshape(words.shape[0], 128, -1), scales


def unpack4(words, scales):
    return unpack_weight(words.reshape(words.shape[0], 128, -1, 2), scales, "e2m1")


B, I, N, L = 512, 512, 1024, 2
SIGSIZE = sum(2 ** k for k in range(1, L + 1))
SAVED = N * (1 + SIGSIZE)


def sigjoin(prev_sigs, disp, time_lapse, level):
    n = prev_sigs.shape[0]
    v = np.concatenate([disp, np.full_like(disp, 1.0) * time_lapse], axis=1)
    seg = [v]
    for k in range(2, level + 1):
        seg.append((seg[-1][:, :, None] * v[:, None, :]).reshape(n, -1) / k)
    S, off = [], 0
    for k in range(1, level + 1):
        sz = 2 ** k
        S.append(prev_sigs[:, off:off + sz])
        off += sz
    out = []
    for k in range(1, level + 1):
        r = S[k - 1] + seg[k - 1]
        for i in range(1, k):
            r = r + (S[i - 1][:, :, None] * seg[k - i - 1][:, None, :]).reshape(n, 2 ** k)
        out.append(r)
    return np.concatenate(out, axis=1)


def setup_inputs():
    s = mx_kscale(I)
    u = mx_kscale(SAVED)
    d = np.minimum(u, 1.0 / u) ** 2
    x = bf(np.random.standard_normal((B, I)) * s)
    prev_sigs = bf(np.random.standard_normal((B, N * SIGSIZE)) * 0.5 * d[:N * SIGSIZE])
    prev_states = bf(np.random.standard_normal((B, N)) * d[N * SIGSIZE:])
    W_w_words, W_w_scales = pack4(np.ascontiguousarray((np.random.standard_normal((N, I)) / np.sqrt(I) / s).T))
    W_b = bf(np.random.standard_normal(N) * 0.1)
    U_w_words, U_w_scales = pack4(np.ascontiguousarray((np.random.standard_normal((N, SAVED)) / np.sqrt(SAVED) / d).T))
    U_b = bf(np.random.standard_normal(N) * 0.1)
    log_timelapse = bf(np.log(0.1) + 0.2 * np.random.standard_normal(1))
    return {"x": x,
            "prev_sigs": prev_sigs,
            "prev_states": prev_states,
            "W_w_words": W_w_words,
            "W_w_scales": W_w_scales,
            "W_b": W_b,
            "U_w_words": U_w_words,
            "U_w_scales": U_w_scales,
            "U_b": U_b,
            "log_timelapse": log_timelapse}


def reference(x, prev_sigs, prev_states, W_w_words, W_w_scales, W_b, U_w_words, U_w_scales, U_b, log_timelapse):
    h = (mxq(f64(x), 1, "e4m3") @ unpack4(W_w_words, W_w_scales)) + f64(W_b)
    mem = np.concatenate([f64(prev_sigs), f64(prev_states)], 1)
    raw = h + (mxq(mem, 1, "e4m3") @ unpack4(U_w_words, U_w_scales)) + f64(U_b)
    disp = (raw - f64(prev_states)).reshape(-1, 1)
    tl = np.exp(f64(log_timelapse))[0]
    sigs = sigjoin(f64(prev_sigs).reshape(-1, SIGSIZE), disp, tl, L)
    sigs = sigs.reshape(-1, N * SIGSIZE)
    return np.concatenate([sigs, raw], axis=1)

@@ -1,0 +1,255 @@
+from contextlib import ExitStack
+
+import concourse.mybir as mybir
+from concourse.masks import make_identity
+
+FLOPS = 2 * 512 * 7680 * 1024
+
+F32 = mybir.dt.float32
+BF16 = mybir.dt.bfloat16
+U8 = mybir.dt.uint8
+U32 = mybir.dt.uint32
+I32 = mybir.dt.int32
+FP8X4 = mybir.dt.float8_e4m3fn_x4
+FP4X4 = mybir.dt.float4_e2m1fn_x4
+ALU = mybir.AluOpType
+ACT = mybir.ActivationFunctionType
+
+P = 128
+NPASS = 15
+HALF = 512
+CHUNKS = [(0, 4), (4, 4), (8, 4), (12, 2), (14, 1)]
+UNITS = [(0, 0), (1, 0), (0, 1), (2, 0), (1, 1), (3, 0), (2, 1), (3, 1)]
+
+
+def tile_recurrentsig_kernel(
+    tc, x, prev_sigs, prev_states, W_w_words, W_w_scales, W_b, U_w_words, U_w_scales, U_b, log_timelapse, out
+):
+    nc = tc.nc
+    with ExitStack() as ctx:
+        keep = ctx.enter_context(tc.tile_pool(name="keep", bufs=1))
+        stage = ctx.enter_context(tc.tile_pool(name="stage", bufs=3))
+        outp = ctx.enter_context(tc.tile_pool(name="outp", bufs=4))
+        rawp = ctx.enter_context(tc.tile_pool(name="rawp", bufs=3))
+        ps_tr = ctx.enter_context(tc.psum_pool(name="ps_tr", bufs=4))
+        ps_acc = ctx.enter_context(tc.psum_pool(name="ps_acc", bufs=4))
+        ctx.enter_context(tc.manual_schedule())
+
+        wscl = [keep.tile([P, NPASS, HALF], U8, name="wscl%d" % h, align_bytes=64) for h in range(2)]
+        ww = [keep.tile([P, NPASS, 1024], U8, name="ww%d" % h, align_bytes=64) for h in range(2)]
+        memt = [keep.tile([P, 7680], BF16, name="mem%d" % m, align_bytes=64) for m in range(4)]
+        codes = [keep.tile([P, NPASS * P], U32, name="codes%d" % m, align_bytes=64) for m in range(4)]
+        ascl = [keep.tile([P, NPASS * P], U8, name="ascl%d" % m, align_bytes=64) for m in range(4)]
+        ident = keep.tile([P, P], F32, name="ident")
+        ones = keep.tile([P, P], BF16, name="ones")
+        zb = keep.tile([P, 1024], BF16, name="zb")
+        beta = keep.tile([P, 1024], F32, name="beta")
+        ltb = keep.tile([P, 1], BF16, name="ltb")
+        tl = keep.tile([P, 1], F32, name="tl")
+        htl = keep.tile([P, 1], F32, name="htl")
+        qtl = keep.tile([P, 1], F32, name="qtl")
+        ypl = [keep.tile([P, 6, HALF], F32, name="ypl%d" % b) for b in range(2)]
+        upl = [keep.tile([P, 2, HALF], F32, name="upl%d" % b) for b in range(2)]
+
+        make_identity(nc, ident[:])
+        nc.vector.memset(zb[:], 0.0)
+        nc.vector.memset(ones[:], 1.0)
+        for h in range(2):
+            nc.vector.memset(wscl[h][:].rearrange("p g n -> p (g n)").bitcast(I32), 0)
+        nc.sync.dma_start(out=ltb[:], in_=log_timelapse.partition_broadcast(P))
+
+        def load_mem(m):
+            rows = slice(P * m, P * m + P)
+            nc.sync.dma_start(out=memt[m][:, 0:512], in_=x[rows, :])
+            for c0, c1 in ((0, 1536), (1536, 3584), (3584, 5632), (5632, 6144)):
+                nc.sync.dma_start(out=memt[m][:, 512 + c0 : 512 + c1], in_=prev_sigs[rows, c0:c1])
+            nc.sync.dma_start(out=memt[m][:, 6656:7680], in_=prev_states[rows, :])
+
+        def load_scales(h):
+            cols = slice(HALF * h, HALF * h + HALF)
+            for b in range(2):
+                for r in range(4):
+                    nc.sync.dma_start(
+                        out=wscl[h][32 * b + r : P : 64, 1:NPASS, :].bitcast(I32),
+                        in_=U_w_scales[:, 4 * b + r : 16 : 8, cols].rearrange("g q n -> q g n").bitcast(I32),
+                    )
+            for r in range(4):
+                nc.sync.dma_start(
+                    out=wscl[h][r:P:32, 0, :].bitcast(I32), in_=W_w_scales[0, r:16:4, cols].bitcast(I32)
+                )
+
+        def load_words(h):
+            cols = slice(1024 * h, 1024 * h + 1024)
+            nc.sync.dma_start(out=ww[h][:, 0, :].bitcast(I32), in_=W_w_words[0, :, cols].bitcast(I32))
+            for g0, g1 in ((0, 3), (3, 7), (7, 11), (11, 14)):
+                nc.sync.dma_start(
+                    out=ww[h][:, 1 + g0 : 1 + g1, :].bitcast(I32),
+                    in_=U_w_words[g0:g1, :, cols].rearrange("g p n -> p g n").bitcast(I32),
+                )
+
+        load_mem(0)
+        nc.sync.dma_start(out=zb[0:1, :], in_=W_b.rearrange("(o n) -> o n", o=1))
+        nc.sync.dma_start(out=zb[1:2, :], in_=U_b.rearrange("(o n) -> o n", o=1))
+        load_scales(0)
+        load_words(0)
+        load_mem(1)
+        load_scales(1)
+        load_words(1)
+        load_mem(2)
+
+        def prep(m, k):
+            g0, n = CHUNKS[k]
+            memw = memt[m][:].bitcast(F32)
+            gs = stage.tile([P, 2048], BF16, name="gs", align_bytes=64)
+            gsf = gs[:].bitcast(F32).rearrange("p (g r u) -> p g r u", g=4, u=2)
+            for b0 in range(0, n, 2):
+                nb = min(2, n - b0)
+                tr = ps_tr.tile([P, 2, 2, P], F32, name="tr")
+                for gg in range(nb):
+                    g = g0 + b0 + gg
+                    for u in range(2):
+                        nc.tensor.transpose(tr[:, gg, u, :], memw[:, 256 * g + u : 256 * (g + 1) : 2], ident[:])
+                nc.scalar.copy(
+                    out=gsf[:, b0 : b0 + nb, :, :], in_=tr[:, 0:nb, :, :].rearrange("p g u r -> p g r u")
+                )
+            nc.vector.quantize_mx(
+                out=codes[m][:, P * g0 : P * (g0 + n)].bitcast(FP8X4),
+                scales=ascl[m][:, P * g0 : P * (g0 + n)],
+                in_=gs[:, 0 : 512 * n],
+            )
+
+        accs = {}
+
+        def mx(i):
+            m, h = UNITS[i]
+            acc = ps_acc.tile([P, HALF], F32, name="acc")
+            accs[i] = acc
+            for g in range(NPASS):
+                nc.tensor.matmul_mx(
+                    out=acc[:],
+                    lhsT=codes[m][:, P * g : P * (g + 1)].bitcast(FP8X4),
+                    lhsT_scale=ascl[m][:, P * g : P * (g + 1)],
+                    rhs=ww[h][:, g, :].bitcast(FP4X4),
+                    rhs_scale=wscl[h][:, g, :],
+                    start=(g == 0),
+                    stop=(g == NPASS - 1),
+                )
+
+        def sig_view(i):
+            m, h = UNITS[i]
+            return memt[m][:, 512 + 3072 * h : 512 + 3072 * (h + 1)].rearrange("p (n c) -> p n c", c=6)
+
+        def s_pre(i):
+            b = i % 2
+            a1 = sig_view(i)[:, :, 1]
+            nc.scalar.activation(out=upl[b][:, 1, :], in_=a1, func=ACT.Identity, bias=htl[:, 0:1], scale=1.0)
+            nc.scalar.activation(out=ypl[b][:, 5, :], in_=a1, func=ACT.Identity, bias=qtl[:, 0:1], scale=tl[:, 0:1])
+
+        raws = {}
+
+        def v_raw(i):
+            m, h = UNITS[i]
+            rt = rawp.tile([P, HALF], F32, name="rt")
+            raws[i] = rt
+            nc.vector.tensor_tensor(out=rt[:], in0=accs[i][:], in1=beta[:, HALF * h : HALF * (h + 1)], op=ALU.add)
+            nc.sync.dma_start(out=out[P * m : P * m + P, 6144 + HALF * h : 6144 + HALF * (h + 1)], in_=rt[:])
+
+        def v_d(i):
+            m, h = UNITS[i]
+            nc.vector.tensor_tensor(
+                out=ypl[i % 2][:, 0, :],
+                in0=raws[i][:],
+                in1=memt[m][:, 6656 + HALF * h : 6656 + HALF * (h + 1)],
+                op=ALU.subtract,
+            )
+
+        def v_u0(i):
+            b = i % 2
+            nc.vector.scalar_tensor_tensor(
+                out=upl[b][:, 0, :], in0=ypl[b][:, 0, :], scalar=0.5, in1=sig_view(i)[:, :, 0], op0=ALU.mult, op1=ALU.add
+            )
+            nc.scalar.mul(out=ypl[b][:, 3, :], in_=upl[b][:, 0, :], mul=tl[:, 0:1])
+
+        def v_y24(i):
+            b = i % 2
+            for w in range(2):
+                nc.vector.tensor_tensor(
+                    out=ypl[b][:, 2 + 2 * w, :], in0=ypl[b][:, 0, :], in1=upl[b][:, w, :], op=ALU.mult
+                )
+
+        def v_final(i, j):
+            m, h = UNITS[i]
+            ot = outp.tile([P, 256, 6], F32, name="ot")
+            nc.vector.tensor_tensor(
+                out=ot[:],
+                in0=sig_view(i)[:, 256 * j : 256 * (j + 1), :],
+                in1=ypl[i % 2][:, :, 256 * j : 256 * (j + 1)].rearrange("p c n -> p n c"),
+                op=ALU.add,
+            )
+            c0 = 3072 * h + 1536 * j
+            nc.sync.dma_start(out=out[P * m : P * m + P, c0 : c0 + 1536], in_=ot[:].rearrange("p n c -> p (n c)"))
+
+        for k in range(5):
+            prep(0, k)
+        nc.scalar.activation(out=tl[:], in_=ltb[:], func=ACT.Exp)
+        nc.vector.tensor_scalar_mul(out=htl[:], in0=tl[:], scalar1=0.5)
+        nc.vector.tensor_tensor(out=qtl[:], in0=tl[:], in1=htl[:], op=ALU.mult)
+        for b in range(2):
+            nc.vector.tensor_copy(out=ypl[b][:, 1, :], in_=tl[:, 0:1].to_broadcast([P, HALF]))
+        for h in range(2):
+            bb = ps_acc.tile([P, HALF], F32, name="acc")
+            nc.tensor.matmul(out=bb[:], lhsT=ones[:], rhs=zb[:, HALF * h : HALF * (h + 1)], start=True, stop=True)
+            nc.scalar.copy(out=beta[:, HALF * h : HALF * (h + 1)], in_=bb[:])
+        s_pre(0)
+        mx(0)
+        v_raw(0)
+        v_d(0)
+        v_u0(0)
+        prep(1, 0)
+        v_y24(0)
+        prep(1, 1)
+        v_final(0, 0)
+        prep(1, 2)
+        v_final(0, 1)
+        prep(1, 3)
+        prep(1, 4)
+        load_mem(3)
+        s_pre(1)
+        mx(1)
+        mx(2)
+        v_raw(1)
+        v_d(1)
+        v_u0(1)
+        v_y24(1)
+        for i in range(1, 8):
+            qt = {1: 2, 3: 3}.get(i)
+            last = i == 7
+            if not last:
+                s_pre(i + 1)
+            v_final(i, 0)
+            if qt:
+                prep(qt, 0)
+            if not last:
+                v_raw(i + 1)
+            if qt:
+                prep(qt, 1)
+            v_final(i, 1)
+            if qt:
+                prep(qt, 2)
+            if not last:
+                v_d(i + 1)
+            if qt:
+                prep(qt, 3)
+            if not last:
+                v_u0(i + 1)
+            if qt:
+                prep(qt, 4)
+            if not last:
+                v_y24(i + 1)
+            if i == 1:
+                mx(3)
+                mx(4)
+            if i == 3:
+                mx(5)
+                mx(6)
+                mx(7)

@@ -47,9 +47,8 @@ def tile_recurrentsig_kernel(
         ltb = keep.tile([P, 1], BF16, name="ltb")
         tl = keep.tile([P, 1], F32, name="tl")
         htl = keep.tile([P, 1], F32, name="htl")
-        qtl = keep.tile([P, 1], F32, name="qtl")
         ypl = [keep.tile([P, 6, HALF], F32, name="ypl%d" % b) for b in range(2)]
-        upl = [keep.tile([P, 2, HALF], F32, name="upl%d" % b) for b in range(2)]
+        upl = [keep.tile([P, 3, HALF], F32, name="upl%d" % b) for b in range(2)]
 
         make_identity(nc, ident[:])
         nc.vector.memset(zb[:], 0.0)
@@ -141,9 +140,11 @@ def tile_recurrentsig_kernel(
 
         def s_pre(i):
             b = i % 2
-            a1 = sig_view(i)[:, :, 1]
-            nc.scalar.activation(out=upl[b][:, 1, :], in_=a1, func=ACT.Identity, bias=htl[:, 0:1], scale=1.0)
-            nc.scalar.activation(out=ypl[b][:, 5, :], in_=a1, func=ACT.Identity, bias=qtl[:, 0:1], scale=tl[:, 0:1])
+            nc.scalar.copy(out=upl[b][:, 2, :], in_=sig_view(i)[:, :, 0])
+            nc.scalar.activation(
+                out=upl[b][:, 1, :], in_=sig_view(i)[:, :, 1], func=ACT.Identity, bias=htl[:, 0:1], scale=1.0
+            )
+            nc.scalar.mul(out=ypl[b][:, 5, :], in_=upl[b][:, 1, :], mul=tl[:, 0:1])
 
         raws = {}
 
@@ -166,7 +167,7 @@ def tile_recurrentsig_kernel(
         def v_u0(i):
             b = i % 2
             nc.vector.scalar_tensor_tensor(
-                out=upl[b][:, 0, :], in0=ypl[b][:, 0, :], scalar=0.5, in1=sig_view(i)[:, :, 0], op0=ALU.mult, op1=ALU.add
+                out=upl[b][:, 0, :], in0=ypl[b][:, 0, :], scalar=0.5, in1=upl[b][:, 2, :], op0=ALU.mult, op1=ALU.add
             )
             nc.scalar.mul(out=ypl[b][:, 3, :], in_=upl[b][:, 0, :], mul=tl[:, 0:1])
 
@@ -177,23 +178,32 @@ def tile_recurrentsig_kernel(
                     out=ypl[b][:, 2 + 2 * w, :], in0=ypl[b][:, 0, :], in1=upl[b][:, w, :], op=ALU.mult
                 )
 
-        def v_final(i, j):
+        def v_part(i, n0, nn):
             m, h = UNITS[i]
-            ot = outp.tile([P, 256, 6], F32, name="ot")
+            ot = outp.tile([P, 128, 2, 6], F32, name="ot")
+            c0 = 3072 * h + 6 * n0
             nc.vector.tensor_tensor(
-                out=ot[:],
-                in0=sig_view(i)[:, 256 * j : 256 * (j + 1), :],
-                in1=ypl[i % 2][:, :, 256 * j : 256 * (j + 1)].rearrange("p c n -> p n c"),
+                out=ot[:, 0 : nn // 2, :, :].rearrange("p m t c -> p m c t"),
+                in0=memt[m][:, 512 + c0 : 512 + c0 + 6 * nn].rearrange("p (m t c) -> p m c t", t=2, c=6),
+                in1=ypl[i % 2][:, :, n0 : n0 + nn].rearrange("p c (m t) -> p m c t", t=2),
                 op=ALU.add,
             )
-            c0 = 3072 * h + 1536 * j
-            nc.sync.dma_start(out=out[P * m : P * m + P, c0 : c0 + 1536], in_=ot[:].rearrange("p n c -> p (n c)"))
+            nc.sync.dma_start(
+                out=out[P * m : P * m + P, c0 : c0 + 6 * nn],
+                in_=ot[:, 0 : nn // 2, :, :].rearrange("p m t c -> p (m t c)"),
+            )
+
+        def v_final(i, j):
+            if i == 7 and j == 1:
+                v_part(i, 256, 128)
+                v_part(i, 384, 128)
+            else:
+                v_part(i, 256 * j, 256)
 
         for k in range(5):
             prep(0, k)
         nc.scalar.activation(out=tl[:], in_=ltb[:], func=ACT.Exp)
         nc.vector.tensor_scalar_mul(out=htl[:], in0=tl[:], scalar1=0.5)
-        nc.vector.tensor_tensor(out=qtl[:], in0=tl[:], in1=htl[:], op=ALU.mult)
         for b in range(2):
             nc.vector.tensor_copy(out=ypl[b][:, 1, :], in_=tl[:, 0:1].to_broadcast([P, HALF]))
         for h in range(2):

@@ -55,7 +55,9 @@ def tile_recurrentsig_kernel(
         nc.vector.memset(ones[:], 1.0)
         for h in range(2):
             nc.vector.memset(wscl[h][:].rearrange("p g n -> p (g n)").bitcast(I32), 0)
-        nc.sync.dma_start(out=ltb[:], in_=log_timelapse.partition_broadcast(P))
+        nc.scalar.dma_start(out=ltb[:], in_=log_timelapse.partition_broadcast(P))
+        nc.scalar.dma_start(out=zb[0:1, :], in_=W_b.rearrange("(o n) -> o n", o=1))
+        nc.scalar.dma_start(out=zb[1:2, :], in_=U_b.rearrange("(o n) -> o n", o=1))
 
         def load_mem(m):
             rows = slice(P * m, P * m + P)
@@ -87,8 +89,6 @@ def tile_recurrentsig_kernel(
                 )
 
         load_mem(0)
-        nc.sync.dma_start(out=zb[0:1, :], in_=W_b.rearrange("(o n) -> o n", o=1))
-        nc.sync.dma_start(out=zb[1:2, :], in_=U_b.rearrange("(o n) -> o n", o=1))
         load_scales(0)
         load_words(0)
         load_mem(1)
@@ -96,7 +96,9 @@ def tile_recurrentsig_kernel(
         load_words(1)
         load_mem(2)
 
-        def prep(m, k):
+        staged = {}
+
+        def prep_ts(m, k):
             g0, n = CHUNKS[k]
             memw = memt[m][:].bitcast(F32)
             gs = stage.tile([P, 2048], BF16, name="gs", align_bytes=64)
@@ -111,6 +113,11 @@ def tile_recurrentsig_kernel(
                 nc.scalar.copy(
                     out=gsf[:, b0 : b0 + nb, :, :], in_=tr[:, 0:nb, :, :].rearrange("p g u r -> p g r u")
                 )
+            staged[(m, k)] = gs
+
+        def quant(m, k):
+            g0, n = CHUNKS[k]
+            gs = staged[(m, k)]
             nc.vector.quantize_mx(
                 out=codes[m][:, P * g0 : P * (g0 + n)].bitcast(FP8X4),
                 scales=ascl[m][:, P * g0 : P * (g0 + n)],
@@ -201,7 +208,8 @@ def tile_recurrentsig_kernel(
                 v_part(i, 256 * j, 256)
 
         for k in range(5):
-            prep(0, k)
+            prep_ts(0, k)
+            quant(0, k)
         nc.scalar.activation(out=tl[:], in_=ltb[:], func=ACT.Exp)
         nc.vector.tensor_scalar_mul(out=htl[:], in0=tl[:], scalar1=0.5)
         for b in range(2):
@@ -214,15 +222,20 @@ def tile_recurrentsig_kernel(
         mx(0)
         v_raw(0)
         v_d(0)
+        prep_ts(1, 0)
         v_u0(0)
-        prep(1, 0)
+        prep_ts(1, 1)
         v_y24(0)
-        prep(1, 1)
+        quant(1, 0)
+        prep_ts(1, 2)
         v_final(0, 0)
-        prep(1, 2)
+        quant(1, 1)
+        quant(1, 2)
+        prep_ts(1, 3)
+        prep_ts(1, 4)
         v_final(0, 1)
-        prep(1, 3)
-        prep(1, 4)
+        quant(1, 3)
+        quant(1, 4)
         load_mem(3)
         s_pre(1)
         mx(1)
@@ -236,26 +249,30 @@ def tile_recurrentsig_kernel(
             last = i == 7
             if not last:
                 s_pre(i + 1)
-            v_final(i, 0)
             if qt:
-                prep(qt, 0)
+                for k in range(3):
+                    prep_ts(qt, k)
+            v_final(i, 0)
             if not last:
                 v_raw(i + 1)
-            if qt:
-                prep(qt, 1)
             v_final(i, 1)
             if qt:
-                prep(qt, 2)
+                quant(qt, 0)
+                prep_ts(qt, 3)
             if not last:
                 v_d(i + 1)
             if qt:
-                prep(qt, 3)
+                quant(qt, 1)
+                prep_ts(qt, 4)
             if not last:
                 v_u0(i + 1)
             if qt:
-                prep(qt, 4)
+                quant(qt, 2)
             if not last:
                 v_y24(i + 1)
+            if qt:
+                quant(qt, 3)
+                quant(qt, 4)
             if i == 1:
                 mx(3)
                 mx(4)

@@ -35,7 +35,8 @@ def tile_recurrentsig_kernel(
         ps_acc = ctx.enter_context(tc.psum_pool(name="ps_acc", bufs=4))
         ctx.enter_context(tc.manual_schedule())
 
-        wscl = [keep.tile([P, NPASS, HALF], U8, name="wscl%d" % h, align_bytes=64) for h in range(2)]
+        wscl = [keep.tile([P, NPASS - 1, HALF], U8, name="wscl%d" % h, align_bytes=64) for h in range(2)]
+        wscl_x = keep.tile([P, 2 * HALF], U8, name="wscl_x", align_bytes=64)
         ww = [keep.tile([P, NPASS, 1024], U8, name="ww%d" % h, align_bytes=64) for h in range(2)]
         memt = [keep.tile([P, 7680], BF16, name="mem%d" % m, align_bytes=64) for m in range(4)]
         codes = [keep.tile([P, NPASS * P], U32, name="codes%d" % m, align_bytes=64) for m in range(4)]
@@ -53,6 +54,7 @@ def tile_recurrentsig_kernel(
         make_identity(nc, ident[:])
         nc.vector.memset(zb[:], 0.0)
         nc.vector.memset(ones[:], 1.0)
+        nc.vector.memset(wscl_x[:].bitcast(I32), 0)
         for h in range(2):
             nc.vector.memset(wscl[h][:].rearrange("p g n -> p (g n)").bitcast(I32), 0)
         nc.scalar.dma_start(out=ltb[:], in_=log_timelapse.partition_broadcast(P))
@@ -71,18 +73,17 @@ def tile_recurrentsig_kernel(
             for b in range(2):
                 for r in range(4):
                     nc.sync.dma_start(
-                        out=wscl[h][32 * b + r : P : 64, 1:NPASS, :].bitcast(I32),
+                        out=wscl[h][32 * b + r : P : 64, :, :].bitcast(I32),
                         in_=U_w_scales[:, 4 * b + r : 16 : 8, cols].rearrange("g q n -> q g n").bitcast(I32),
                     )
-            for r in range(4):
-                nc.sync.dma_start(
-                    out=wscl[h][r:P:32, 0, :].bitcast(I32), in_=W_w_scales[0, r:16:4, cols].bitcast(I32)
-                )
+            if h == 0:
+                for r in range(4):
+                    nc.sync.dma_start(out=wscl_x[r:P:32, :].bitcast(I32), in_=W_w_scales[0, r:16:4, :].bitcast(I32))
 
         def load_words(h):
             cols = slice(1024 * h, 1024 * h + 1024)
             nc.sync.dma_start(out=ww[h][:, 0, :].bitcast(I32), in_=W_w_words[0, :, cols].bitcast(I32))
-            for g0, g1 in ((0, 3), (3, 7), (7, 11), (11, 14)):
+            for g0, g1 in ((0, 3), (3, 7), (7, 11), (11, 13), (13, 14)):
                 nc.sync.dma_start(
                     out=ww[h][:, 1 + g0 : 1 + g1, :].bitcast(I32),
                     in_=U_w_words[g0:g1, :, cols].rearrange("g p n -> p g n").bitcast(I32),
@@ -136,7 +137,7 @@ def tile_recurrentsig_kernel(
                     lhsT=codes[m][:, P * g : P * (g + 1)].bitcast(FP8X4),
                     lhsT_scale=ascl[m][:, P * g : P * (g + 1)],
                     rhs=ww[h][:, g, :].bitcast(FP4X4),
-                    rhs_scale=wscl[h][:, g, :],
+                    rhs_scale=(wscl_x[:, HALF * h : HALF * (h + 1)] if g == 0 else wscl[h][:, g - 1, :]),
                     start=(g == 0),
                     stop=(g == NPASS - 1),
                 )
@@ -203,7 +204,8 @@ def tile_recurrentsig_kernel(
         def v_final(i, j):
             if i == 7 and j == 1:
                 v_part(i, 256, 128)
-                v_part(i, 384, 128)
+                v_part(i, 384, 64)
+                v_part(i, 448, 64)
             else:
                 v_part(i, 256 * j, 256)
 
@@ -233,9 +235,9 @@ def tile_recurrentsig_kernel(
         quant(1, 2)
         prep_ts(1, 3)
         prep_ts(1, 4)
-        v_final(0, 1)
         quant(1, 3)
         quant(1, 4)
+        v_final(0, 1)
         load_mem(3)
         s_pre(1)
         mx(1)

@@ -16,10 +16,24 @@ ALU = mybir.AluOpType
 ACT = mybir.ActivationFunctionType
 
 P = 128
-NPASS = 15
+BATCH_TILES = 4
+PASSES = 15
 HALF = 512
+SIG = 6
+X_COLS = 512
+STATE_COL = X_COLS + 1024 * SIG
 CHUNKS = [(0, 4), (4, 4), (8, 4), (12, 2), (14, 1)]
-UNITS = [(0, 0), (1, 0), (0, 1), (2, 0), (1, 1), (3, 0), (2, 1), (3, 1)]
+SIG_LOADS = ((0, 1536), (1536, 3584), (3584, 5632), (5632, 6144))
+WORD_LOADS = ((0, 3), (3, 7), (7, 11), (11, 13), (13, 14))
+UNITS = [(0, 0), (1, 0), (0, 1), (1, 1), (2, 0), (3, 0), (2, 1), (3, 1)]
+LAST = len(UNITS) - 1
+PREPARED_DURING = {1: 2, 2: 3}
+VIA_PSUM = (3, 4, 5)
+ON_GPSIMD = (4, 5, 6)
+PRODUCTS_BEFORE = {1: (3,)}
+PRODUCTS_AFTER = {1: (4,), 2: (5,), 3: (6,), 4: (7,)}
+PARTS = (((0, 256),), ((256, 256),))
+PARTS_OF_LAST = (((0, 256),), ((256, 128), (384, 64), (448, 64)))
 
 
 def tile_recurrentsig_kernel(
@@ -31,254 +45,307 @@ def tile_recurrentsig_kernel(
         stage = ctx.enter_context(tc.tile_pool(name="stage", bufs=3))
         outp = ctx.enter_context(tc.tile_pool(name="outp", bufs=4))
         rawp = ctx.enter_context(tc.tile_pool(name="rawp", bufs=3))
-        ps_tr = ctx.enter_context(tc.psum_pool(name="ps_tr", bufs=4))
-        ps_acc = ctx.enter_context(tc.psum_pool(name="ps_acc", bufs=4))
+        ps_tr = ctx.enter_context(tc.psum_pool(name="ps_tr", bufs=5))
+        ps_acc = ctx.enter_context(tc.psum_pool(name="ps_acc", bufs=3))
         ctx.enter_context(tc.manual_schedule())
 
-        wscl = [keep.tile([P, NPASS - 1, HALF], U8, name="wscl%d" % h, align_bytes=64) for h in range(2)]
-        wscl_x = keep.tile([P, 2 * HALF], U8, name="wscl_x", align_bytes=64)
-        ww = [keep.tile([P, NPASS, 1024], U8, name="ww%d" % h, align_bytes=64) for h in range(2)]
-        memt = [keep.tile([P, 7680], BF16, name="mem%d" % m, align_bytes=64) for m in range(4)]
-        codes = [keep.tile([P, NPASS * P], U32, name="codes%d" % m, align_bytes=64) for m in range(4)]
-        ascl = [keep.tile([P, NPASS * P], U8, name="ascl%d" % m, align_bytes=64) for m in range(4)]
+        u_scales = [keep.tile([P, PASSES - 1, HALF], U8, name="wscl%d" % h, align_bytes=64) for h in range(2)]
+        w_scales = keep.tile([P, 2 * HALF], U8, name="wscl_x", align_bytes=64)
+        words = [keep.tile([P, PASSES, 2 * HALF], U8, name="ww%d" % h, align_bytes=64) for h in range(2)]
+        rows_in = [keep.tile([P, 512 * PASSES], BF16, name="mem%d" % m, align_bytes=64) for m in range(BATCH_TILES)]
+        codes = [keep.tile([P, PASSES * P], U32, name="codes%d" % m, align_bytes=64) for m in range(BATCH_TILES)]
+        act_scales = [keep.tile([P, PASSES * P], U8, name="ascl%d" % m, align_bytes=64) for m in range(BATCH_TILES)]
         ident = keep.tile([P, P], F32, name="ident")
+        ident_bf = keep.tile([P, P], BF16, name="identb")
         ones = keep.tile([P, P], BF16, name="ones")
-        zb = keep.tile([P, 1024], BF16, name="zb")
-        beta = keep.tile([P, 1024], F32, name="beta")
-        ltb = keep.tile([P, 1], BF16, name="ltb")
+        bias_rows = keep.tile([P, 2 * HALF], BF16, name="zb")
+        bias = keep.tile([P, 2 * HALF], F32, name="beta")
+        log_tl = keep.tile([P, 1], BF16, name="ltb")
         tl = keep.tile([P, 1], F32, name="tl")
-        htl = keep.tile([P, 1], F32, name="htl")
-        ypl = [keep.tile([P, 6, HALF], F32, name="ypl%d" % b) for b in range(2)]
-        upl = [keep.tile([P, 3, HALF], F32, name="upl%d" % b) for b in range(2)]
+        half_tl = keep.tile([P, 1], F32, name="htl")
+        y = [keep.tile([P, SIG, HALF], F32, name="ypl%d" % b) for b in range(2)]
+        aux = [keep.tile([P, 4, HALF], F32, name="upl%d" % b) for b in range(2)]
 
         make_identity(nc, ident[:])
-        nc.vector.memset(zb[:], 0.0)
+        make_identity(nc, ident_bf[:])
+        nc.vector.memset(bias_rows[:], 0.0)
         nc.vector.memset(ones[:], 1.0)
-        nc.vector.memset(wscl_x[:].bitcast(I32), 0)
+        nc.vector.memset(w_scales[:].bitcast(I32), 0)
         for h in range(2):
-            nc.vector.memset(wscl[h][:].rearrange("p g n -> p (g n)").bitcast(I32), 0)
-        nc.scalar.dma_start(out=ltb[:], in_=log_timelapse.partition_broadcast(P))
-        nc.scalar.dma_start(out=zb[0:1, :], in_=W_b.rearrange("(o n) -> o n", o=1))
-        nc.scalar.dma_start(out=zb[1:2, :], in_=U_b.rearrange("(o n) -> o n", o=1))
+            nc.vector.memset(u_scales[h][:].rearrange("p g n -> p (g n)").bitcast(I32), 0)
+        nc.scalar.dma_start(out=log_tl[:], in_=log_timelapse.partition_broadcast(P))
+        nc.scalar.dma_start(out=bias_rows[0:1, :], in_=W_b.rearrange("(o n) -> o n", o=1))
+        nc.scalar.dma_start(out=bias_rows[1:2, :], in_=U_b.rearrange("(o n) -> o n", o=1))
 
-        def load_mem(m):
+        def load_rows(m):
             rows = slice(P * m, P * m + P)
-            nc.sync.dma_start(out=memt[m][:, 0:512], in_=x[rows, :])
-            for c0, c1 in ((0, 1536), (1536, 3584), (3584, 5632), (5632, 6144)):
-                nc.sync.dma_start(out=memt[m][:, 512 + c0 : 512 + c1], in_=prev_sigs[rows, c0:c1])
-            nc.sync.dma_start(out=memt[m][:, 6656:7680], in_=prev_states[rows, :])
+            nc.sync.dma_start(out=rows_in[m][:, 0:X_COLS], in_=x[rows, :])
+            for c0, c1 in SIG_LOADS:
+                nc.sync.dma_start(out=rows_in[m][:, X_COLS + c0 : X_COLS + c1], in_=prev_sigs[rows, c0:c1])
+            nc.sync.dma_start(out=rows_in[m][:, STATE_COL : 512 * PASSES], in_=prev_states[rows, :])
 
         def load_scales(h):
             cols = slice(HALF * h, HALF * h + HALF)
             for b in range(2):
                 for r in range(4):
                     nc.sync.dma_start(
-                        out=wscl[h][32 * b + r : P : 64, :, :].bitcast(I32),
+                        out=u_scales[h][32 * b + r : P : 64, :, :].bitcast(I32),
                         in_=U_w_scales[:, 4 * b + r : 16 : 8, cols].rearrange("g q n -> q g n").bitcast(I32),
                     )
             if h == 0:
                 for r in range(4):
-                    nc.sync.dma_start(out=wscl_x[r:P:32, :].bitcast(I32), in_=W_w_scales[0, r:16:4, :].bitcast(I32))
+                    nc.sync.dma_start(out=w_scales[r:P:32, :].bitcast(I32), in_=W_w_scales[0, r:16:4, :].bitcast(I32))
 
         def load_words(h):
-            cols = slice(1024 * h, 1024 * h + 1024)
-            nc.sync.dma_start(out=ww[h][:, 0, :].bitcast(I32), in_=W_w_words[0, :, cols].bitcast(I32))
-            for g0, g1 in ((0, 3), (3, 7), (7, 11), (11, 13), (13, 14)):
+            cols = slice(2 * HALF * h, 2 * HALF * h + 2 * HALF)
+            nc.sync.dma_start(out=words[h][:, 0, :].bitcast(I32), in_=W_w_words[0, :, cols].bitcast(I32))
+            for g0, g1 in WORD_LOADS:
                 nc.sync.dma_start(
-                    out=ww[h][:, 1 + g0 : 1 + g1, :].bitcast(I32),
+                    out=words[h][:, 1 + g0 : 1 + g1, :].bitcast(I32),
                     in_=U_w_words[g0:g1, :, cols].rearrange("g p n -> p g n").bitcast(I32),
                 )
 
-        load_mem(0)
+        load_rows(0)
         load_scales(0)
         load_words(0)
-        load_mem(1)
+        load_rows(1)
         load_scales(1)
         load_words(1)
-        load_mem(2)
+        load_rows(2)
 
-        staged = {}
+        regrouped = {}
 
-        def prep_ts(m, k):
+        def transpose_chunk(m, k):
             g0, n = CHUNKS[k]
-            memw = memt[m][:].bitcast(F32)
-            gs = stage.tile([P, 2048], BF16, name="gs", align_bytes=64)
-            gsf = gs[:].bitcast(F32).rearrange("p (g r u) -> p g r u", g=4, u=2)
+            row_words = rows_in[m][:].bitcast(F32)
+            grouped = stage.tile([P, 2048], BF16, name="gs", align_bytes=64)
+            grouped_words = grouped[:].bitcast(F32).rearrange("p (g r u) -> p g r u", g=4, u=2)
             for b0 in range(0, n, 2):
                 nb = min(2, n - b0)
-                tr = ps_tr.tile([P, 2, 2, P], F32, name="tr")
+                bank = ps_tr.tile([P, 2, 2, P], F32, name="tr", tag="tr")
                 for gg in range(nb):
                     g = g0 + b0 + gg
                     for u in range(2):
-                        nc.tensor.transpose(tr[:, gg, u, :], memw[:, 256 * g + u : 256 * (g + 1) : 2], ident[:])
+                        nc.tensor.transpose(bank[:, gg, u, :], row_words[:, 256 * g + u : 256 * (g + 1) : 2], ident[:])
                 nc.scalar.copy(
-                    out=gsf[:, b0 : b0 + nb, :, :], in_=tr[:, 0:nb, :, :].rearrange("p g u r -> p g r u")
+                    out=grouped_words[:, b0 : b0 + nb, :, :], in_=bank[:, 0:nb, :, :].rearrange("p g u r -> p g r u")
                 )
-            staged[(m, k)] = gs
+            regrouped[(m, k)] = grouped
 
-        def quant(m, k):
+        def quantise_chunk(m, k):
             g0, n = CHUNKS[k]
-            gs = staged[(m, k)]
             nc.vector.quantize_mx(
                 out=codes[m][:, P * g0 : P * (g0 + n)].bitcast(FP8X4),
-                scales=ascl[m][:, P * g0 : P * (g0 + n)],
-                in_=gs[:, 0 : 512 * n],
+                scales=act_scales[m][:, P * g0 : P * (g0 + n)],
+                in_=regrouped[(m, k)][:, 0 : 512 * n],
             )
 
-        accs = {}
+        products = {}
 
-        def mx(i):
+        def product(i):
             m, h = UNITS[i]
             acc = ps_acc.tile([P, HALF], F32, name="acc")
-            accs[i] = acc
-            for g in range(NPASS):
+            products[i] = acc
+            for g in range(PASSES):
                 nc.tensor.matmul_mx(
                     out=acc[:],
                     lhsT=codes[m][:, P * g : P * (g + 1)].bitcast(FP8X4),
-                    lhsT_scale=ascl[m][:, P * g : P * (g + 1)],
-                    rhs=ww[h][:, g, :].bitcast(FP4X4),
-                    rhs_scale=(wscl_x[:, HALF * h : HALF * (h + 1)] if g == 0 else wscl[h][:, g - 1, :]),
+                    lhsT_scale=act_scales[m][:, P * g : P * (g + 1)],
+                    rhs=words[h][:, g, :].bitcast(FP4X4),
+                    rhs_scale=(w_scales[:, HALF * h : HALF * (h + 1)] if g == 0 else u_scales[h][:, g - 1, :]),
                     start=(g == 0),
-                    stop=(g == NPASS - 1),
+                    stop=(g == PASSES - 1),
                 )
 
-        def sig_view(i):
+        def old_sigs(i):
             m, h = UNITS[i]
-            return memt[m][:, 512 + 3072 * h : 512 + 3072 * (h + 1)].rearrange("p (n c) -> p n c", c=6)
+            c0 = X_COLS + SIG * HALF * h
+            return rows_in[m][:, c0 : c0 + SIG * HALF].rearrange("p (n c) -> p n c", c=SIG)
 
-        def s_pre(i):
+        def from_inputs(i):
             b = i % 2
-            nc.scalar.copy(out=upl[b][:, 2, :], in_=sig_view(i)[:, :, 0])
+            if i in ON_GPSIMD:
+                nc.scalar.mul(out=aux[b][:, 2, :], in_=old_sigs(i)[:, :, 0], mul=2.0)
+            else:
+                nc.scalar.copy(out=aux[b][:, 2, :], in_=old_sigs(i)[:, :, 0])
             nc.scalar.activation(
-                out=upl[b][:, 1, :], in_=sig_view(i)[:, :, 1], func=ACT.Identity, bias=htl[:, 0:1], scale=1.0
+                out=aux[b][:, 1, :], in_=old_sigs(i)[:, :, 1], func=ACT.Identity, bias=half_tl[:, 0:1], scale=1.0
             )
-            nc.scalar.mul(out=ypl[b][:, 5, :], in_=upl[b][:, 1, :], mul=tl[:, 0:1])
+            nc.scalar.mul(out=y[b][:, 5, :], in_=aux[b][:, 1, :], mul=tl[:, 0:1])
 
         raws = {}
 
-        def v_raw(i):
+        def add_bias(i):
             m, h = UNITS[i]
-            rt = rawp.tile([P, HALF], F32, name="rt")
-            raws[i] = rt
-            nc.vector.tensor_tensor(out=rt[:], in0=accs[i][:], in1=beta[:, HALF * h : HALF * (h + 1)], op=ALU.add)
-            nc.sync.dma_start(out=out[P * m : P * m + P, 6144 + HALF * h : 6144 + HALF * (h + 1)], in_=rt[:])
+            raw = rawp.tile([P, HALF], F32, name="rt")
+            raws[i] = raw
+            nc.vector.tensor_tensor(out=raw[:], in0=products[i][:], in1=bias[:, HALF * h : HALF * (h + 1)], op=ALU.add)
+            c0 = 1024 * SIG + HALF * h
+            nc.sync.dma_start(out=out[P * m : P * m + P, c0 : c0 + HALF], in_=raw[:])
 
-        def v_d(i):
+        def displacement(i):
             m, h = UNITS[i]
             nc.vector.tensor_tensor(
-                out=ypl[i % 2][:, 0, :],
+                out=y[i % 2][:, 0, :],
                 in0=raws[i][:],
-                in1=memt[m][:, 6656 + HALF * h : 6656 + HALF * (h + 1)],
+                in1=rows_in[m][:, STATE_COL + HALF * h : STATE_COL + HALF * (h + 1)],
                 op=ALU.subtract,
             )
 
-        def v_u0(i):
+        def level_one(i):
             b = i % 2
             nc.vector.scalar_tensor_tensor(
-                out=upl[b][:, 0, :], in0=ypl[b][:, 0, :], scalar=0.5, in1=upl[b][:, 2, :], op0=ALU.mult, op1=ALU.add
+                out=aux[b][:, 0, :], in0=y[b][:, 0, :], scalar=0.5, in1=aux[b][:, 2, :], op0=ALU.mult, op1=ALU.add
             )
-            nc.scalar.mul(out=ypl[b][:, 3, :], in_=upl[b][:, 0, :], mul=tl[:, 0:1])
+            nc.scalar.mul(out=y[b][:, 3, :], in_=aux[b][:, 0, :], mul=tl[:, 0:1])
 
-        def v_y24(i):
+        def level_two(i):
             b = i % 2
             for w in range(2):
-                nc.vector.tensor_tensor(
-                    out=ypl[b][:, 2 + 2 * w, :], in0=ypl[b][:, 0, :], in1=upl[b][:, w, :], op=ALU.mult
+                nc.vector.tensor_tensor(out=y[b][:, 2 + 2 * w, :], in0=y[b][:, 0, :], in1=aux[b][:, w, :], op=ALU.mult)
+
+        def planes_on_gpsimd(i):
+            b = i % 2
+            nc.gpsimd.tensor_tensor(out=aux[b][:, 0, :], in0=y[b][:, 0, :], in1=aux[b][:, 2, :], op=ALU.add)
+            nc.scalar.mul(out=y[b][:, 3, :], in_=aux[b][:, 0, :], mul=half_tl[:, 0:1])
+            nc.gpsimd.tensor_tensor(out=aux[b][:, 3, :], in0=y[b][:, 0, :], in1=aux[b][:, 0, :], op=ALU.mult)
+            nc.scalar.mul(out=y[b][:, 2, :], in_=aux[b][:, 3, :], mul=0.5)
+            nc.gpsimd.tensor_tensor(out=y[b][:, 4, :], in0=y[b][:, 0, :], in1=aux[b][:, 1, :], op=ALU.mult)
+
+        sig_banks = {}
+
+        def copy_sigs(i, q):
+            m, h = UNITS[i]
+            c0 = X_COLS + SIG * (HALF * h + 128 * q)
+            bank = ps_tr.tile([P, 1024], BF16, name="sp", tag="tr")
+            sig_banks[(i, q)] = bank
+            for a0, a1 in ((0, 512), (512, 768)):
+                nc.tensor.matmul(
+                    out=bank[:, a0:a1], lhsT=ident_bf[:], rhs=rows_in[m][:, c0 + a0 : c0 + a1], start=True, stop=True
                 )
 
-        def v_part(i, n0, nn):
+        out_tiles = {}
+
+        def add_quarter(i, q):
             m, h = UNITS[i]
-            ot = outp.tile([P, 128, 2, 6], F32, name="ot")
-            c0 = 3072 * h + 6 * n0
+            if q % 2 == 0:
+                new_sigs = outp.tile([P, 128, 2, SIG], F32, name="ot")
+                out_tiles[i] = new_sigs
+            new_sigs = out_tiles[i]
+            m0 = 64 * (q % 2)
             nc.vector.tensor_tensor(
-                out=ot[:, 0 : nn // 2, :, :].rearrange("p m t c -> p m c t"),
-                in0=memt[m][:, 512 + c0 : 512 + c0 + 6 * nn].rearrange("p (m t c) -> p m c t", t=2, c=6),
-                in1=ypl[i % 2][:, :, n0 : n0 + nn].rearrange("p c (m t) -> p m c t", t=2),
+                out=new_sigs[:, m0 : m0 + 64, :, :].rearrange("p m t c -> p m c t"),
+                in0=sig_banks[(i, q)][:, 0:768].rearrange("p (m t c) -> p m c t", t=2, c=SIG),
+                in1=y[i % 2][:, :, 128 * q : 128 * (q + 1)].rearrange("p c (m t) -> p m c t", t=2),
                 op=ALU.add,
             )
-            nc.sync.dma_start(
-                out=out[P * m : P * m + P, c0 : c0 + 6 * nn],
-                in_=ot[:, 0 : nn // 2, :, :].rearrange("p m t c -> p (m t c)"),
-            )
+            if q % 2 == 1:
+                c0 = SIG * (HALF * h + 128 * (q - 1))
+                nc.sync.dma_start(
+                    out=out[P * m : P * m + P, c0 : c0 + SIG * 256], in_=new_sigs[:].rearrange("p m t c -> p (m t c)")
+                )
 
-        def v_final(i, j):
-            if i == 7 and j == 1:
-                v_part(i, 256, 128)
-                v_part(i, 384, 64)
-                v_part(i, 448, 64)
-            else:
-                v_part(i, 256 * j, 256)
+        def add_and_store(i, j):
+            m, h = UNITS[i]
+            for n0, nn in (PARTS_OF_LAST if i == LAST else PARTS)[j]:
+                new_sigs = outp.tile([P, 128, 2, SIG], F32, name="ot")
+                c0 = SIG * (HALF * h + n0)
+                nc.vector.tensor_tensor(
+                    out=new_sigs[:, 0 : nn // 2, :, :].rearrange("p m t c -> p m c t"),
+                    in0=rows_in[m][:, X_COLS + c0 : X_COLS + c0 + SIG * nn].rearrange(
+                        "p (m t c) -> p m c t", t=2, c=SIG
+                    ),
+                    in1=y[i % 2][:, :, n0 : n0 + nn].rearrange("p c (m t) -> p m c t", t=2),
+                    op=ALU.add,
+                )
+                nc.sync.dma_start(
+                    out=out[P * m : P * m + P, c0 : c0 + SIG * nn],
+                    in_=new_sigs[:, 0 : nn // 2, :, :].rearrange("p m t c -> p (m t c)"),
+                )
 
-        for k in range(5):
-            prep_ts(0, k)
-            quant(0, k)
-        nc.scalar.activation(out=tl[:], in_=ltb[:], func=ACT.Exp)
-        nc.vector.tensor_scalar_mul(out=htl[:], in0=tl[:], scalar1=0.5)
+        for k in range(len(CHUNKS)):
+            transpose_chunk(0, k)
+            quantise_chunk(0, k)
+        nc.scalar.activation(out=tl[:], in_=log_tl[:], func=ACT.Exp)
+        nc.vector.tensor_scalar_mul(out=half_tl[:], in0=tl[:], scalar1=0.5)
         for b in range(2):
-            nc.vector.tensor_copy(out=ypl[b][:, 1, :], in_=tl[:, 0:1].to_broadcast([P, HALF]))
+            nc.vector.tensor_copy(out=y[b][:, 1, :], in_=tl[:, 0:1].to_broadcast([P, HALF]))
         for h in range(2):
-            bb = ps_acc.tile([P, HALF], F32, name="acc")
-            nc.tensor.matmul(out=bb[:], lhsT=ones[:], rhs=zb[:, HALF * h : HALF * (h + 1)], start=True, stop=True)
-            nc.scalar.copy(out=beta[:, HALF * h : HALF * (h + 1)], in_=bb[:])
-        s_pre(0)
-        mx(0)
-        v_raw(0)
-        v_d(0)
-        prep_ts(1, 0)
-        v_u0(0)
-        prep_ts(1, 1)
-        v_y24(0)
-        quant(1, 0)
-        prep_ts(1, 2)
-        v_final(0, 0)
-        quant(1, 1)
-        quant(1, 2)
-        prep_ts(1, 3)
-        prep_ts(1, 4)
-        quant(1, 3)
-        quant(1, 4)
-        v_final(0, 1)
-        load_mem(3)
-        s_pre(1)
-        mx(1)
-        mx(2)
-        v_raw(1)
-        v_d(1)
-        v_u0(1)
-        v_y24(1)
-        for i in range(1, 8):
-            qt = {1: 2, 3: 3}.get(i)
-            last = i == 7
-            if not last:
-                s_pre(i + 1)
-            if qt:
+            spread = ps_acc.tile([P, HALF], F32, name="acc")
+            nc.tensor.matmul(
+                out=spread[:], lhsT=ones[:], rhs=bias_rows[:, HALF * h : HALF * (h + 1)], start=True, stop=True
+            )
+            nc.scalar.copy(out=bias[:, HALF * h : HALF * (h + 1)], in_=spread[:])
+
+        from_inputs(0)
+        product(0)
+        add_bias(0)
+        displacement(0)
+        transpose_chunk(1, 0)
+        level_one(0)
+        transpose_chunk(1, 1)
+        level_two(0)
+        quantise_chunk(1, 0)
+        transpose_chunk(1, 2)
+        add_and_store(0, 0)
+        quantise_chunk(1, 1)
+        quantise_chunk(1, 2)
+        transpose_chunk(1, 3)
+        transpose_chunk(1, 4)
+        quantise_chunk(1, 3)
+        quantise_chunk(1, 4)
+        add_and_store(0, 1)
+        load_rows(3)
+        from_inputs(1)
+        product(1)
+        product(2)
+        add_bias(1)
+        displacement(1)
+        level_one(1)
+        level_two(1)
+
+        for i in range(1, len(UNITS)):
+            new_tile = PREPARED_DURING.get(i)
+            follower = i < LAST
+            if follower:
+                from_inputs(i + 1)
+            for early in PRODUCTS_BEFORE.get(i, ()):
+                product(early)
+            if new_tile:
                 for k in range(3):
-                    prep_ts(qt, k)
-            v_final(i, 0)
-            if not last:
-                v_raw(i + 1)
-            v_final(i, 1)
-            if qt:
-                quant(qt, 0)
-                prep_ts(qt, 3)
-            if not last:
-                v_d(i + 1)
-            if qt:
-                quant(qt, 1)
-                prep_ts(qt, 4)
-            if not last:
-                v_u0(i + 1)
-            if qt:
-                quant(qt, 2)
-            if not last:
-                v_y24(i + 1)
-            if qt:
-                quant(qt, 3)
-                quant(qt, 4)
-            if i == 1:
-                mx(3)
-                mx(4)
-            if i == 3:
-                mx(5)
-                mx(6)
-                mx(7)
+                    transpose_chunk(new_tile, k)
+            if i in VIA_PSUM:
+                add_bias(i + 1)
+                displacement(i + 1)
+                planes_on_gpsimd(i + 1)
+                for q in range(4):
+                    add_quarter(i, q)
+                    if i + 1 in VIA_PSUM:
+                        copy_sigs(i + 1, q)
+            else:
+                add_and_store(i, 0)
+                if follower:
+                    add_bias(i + 1)
+                add_and_store(i, 1)
+                if new_tile:
+                    quantise_chunk(new_tile, 0)
+                    transpose_chunk(new_tile, 3)
+                if follower:
+                    displacement(i + 1)
+                if new_tile:
+                    quantise_chunk(new_tile, 1)
+                    transpose_chunk(new_tile, 4)
+                if follower:
+                    level_one(i + 1)
+                if new_tile:
+                    quantise_chunk(new_tile, 2)
+                if follower:
+                    level_two(i + 1)
+                if new_tile:
+                    quantise_chunk(new_tile, 3)
+                    quantise_chunk(new_tile, 4)
+            for later in PRODUCTS_AFTER.get(i, ()):
+                product(later)
+            if i + 1 == VIA_PSUM[0]:
+                for q in range(4):
+                    copy_sigs(i + 1, q)

@@ -28,8 +28,8 @@ WORD_LOADS = ((0, 3), (3, 7), (7, 11), (11, 13), (13, 14))
 UNITS = [(0, 0), (1, 0), (0, 1), (1, 1), (2, 0), (3, 0), (2, 1), (3, 1)]
 LAST = len(UNITS) - 1
 PREPARED_DURING = {1: 2, 2: 3}
-VIA_PSUM = (3, 4, 5)
-ON_GPSIMD = (4, 5, 6)
+VIA_PSUM = (3, 4, 5, 6)
+ON_GPSIMD = (4, 5, 6, 7)
 PRODUCTS_BEFORE = {1: (3,)}
 PRODUCTS_AFTER = {1: (4,), 2: (5,), 3: (6,), 4: (7,)}
 PARTS = (((0, 256),), ((256, 256),))
@@ -322,6 +322,14 @@ def tile_recurrentsig_kernel(
                     add_quarter(i, q)
                     if i + 1 in VIA_PSUM:
                         copy_sigs(i + 1, q)
+                if new_tile:
+                    quantise_chunk(new_tile, 0)
+                    transpose_chunk(new_tile, 3)
+                    quantise_chunk(new_tile, 1)
+                    transpose_chunk(new_tile, 4)
+                    quantise_chunk(new_tile, 2)
+                    quantise_chunk(new_tile, 3)
+                    quantise_chunk(new_tile, 4)
             else:
                 add_and_store(i, 0)
                 if follower:

@@ -86,12 +86,11 @@ def tile_recurrentsig_kernel(
 
         def load_scales(h):
             cols = slice(HALF * h, HALF * h + HALF)
-            for b in range(2):
-                for r in range(4):
-                    nc.sync.dma_start(
-                        out=u_scales[h][32 * b + r : P : 64, :, :].bitcast(I32),
-                        in_=U_w_scales[:, 4 * b + r : 16 : 8, cols].rearrange("g q n -> q g n").bitcast(I32),
-                    )
+            for r in range(4):
+                nc.sync.dma_start(
+                    out=u_scales[h][r : P : 32, :, :].bitcast(I32),
+                    in_=U_w_scales[:, r : 16 : 4, cols].rearrange("g q n -> q g n").bitcast(I32),
+                )
             if h == 0:
                 for r in range(4):
                     nc.sync.dma_start(out=w_scales[r:P:32, :].bitcast(I32), in_=W_w_scales[0, r:16:4, :].bitcast(I32))

@@ -28,8 +28,8 @@ WORD_LOADS = ((0, 3), (3, 7), (7, 11), (11, 13), (13, 14))
 UNITS = [(0, 0), (1, 0), (0, 1), (1, 1), (2, 0), (3, 0), (2, 1), (3, 1)]
 LAST = len(UNITS) - 1
 PREPARED_DURING = {1: 2, 2: 3}
-VIA_PSUM = (3, 4, 5, 6)
-ON_GPSIMD = (4, 5, 6, 7)
+FED = (0, 4, 5, 6,)
+ON_GPSIMD = (1, 5, 6, 7,)
 PRODUCTS_BEFORE = {1: (3,)}
 PRODUCTS_AFTER = {1: (4,), 2: (5,), 3: (6,), 4: (7,)}
 PARTS = (((0, 256),), ((256, 256),))
@@ -105,9 +105,9 @@ def tile_recurrentsig_kernel(
                 )
 
         load_rows(0)
+        load_rows(1)
         load_scales(0)
         load_words(0)
-        load_rows(1)
         load_scales(1)
         load_words(1)
         load_rows(2)
@@ -225,6 +225,21 @@ def tile_recurrentsig_kernel(
 
         out_tiles = {}
 
+        def add_tail(i, n0, nn):
+            m, h = UNITS[i]
+            new_sigs = outp.tile([P, 128, 2, SIG], F32, name="ot")
+            c0 = SIG * (HALF * h + n0)
+            nc.vector.tensor_tensor(
+                out=new_sigs[:, 0 : nn // 2, :, :].rearrange("p m t c -> p m c t"),
+                in0=rows_in[m][:, X_COLS + c0 : X_COLS + c0 + SIG * nn].rearrange("p (m t c) -> p m c t", t=2, c=SIG),
+                in1=y[i % 2][:, :, n0 : n0 + nn].rearrange("p c (m t) -> p m c t", t=2),
+                op=ALU.add,
+            )
+            nc.sync.dma_start(
+                out=out[P * m : P * m + P, c0 : c0 + SIG * nn],
+                in_=new_sigs[:, 0 : nn // 2, :, :].rearrange("p m t c -> p (m t c)"),
+            )
+
         def add_quarter(i, q):
             m, h = UNITS[i]
             if q % 2 == 0:
@@ -232,9 +247,11 @@ def tile_recurrentsig_kernel(
                 out_tiles[i] = new_sigs
             new_sigs = out_tiles[i]
             m0 = 64 * (q % 2)
+            s0 = X_COLS + SIG * (HALF * h + 128 * q)
+            old = sig_banks[(i, q)][:, 0:768] if i in FED else rows_in[m][:, s0 : s0 + 768]
             nc.vector.tensor_tensor(
                 out=new_sigs[:, m0 : m0 + 64, :, :].rearrange("p m t c -> p m c t"),
-                in0=sig_banks[(i, q)][:, 0:768].rearrange("p (m t c) -> p m c t", t=2, c=SIG),
+                in0=old.rearrange("p (m t c) -> p m c t", t=2, c=SIG),
                 in1=y[i % 2][:, :, 128 * q : 128 * (q + 1)].rearrange("p c (m t) -> p m c t", t=2),
                 op=ALU.add,
             )
@@ -262,10 +279,10 @@ def tile_recurrentsig_kernel(
                     in_=new_sigs[:, 0 : nn // 2, :, :].rearrange("p m t c -> p (m t c)"),
                 )
 
+        nc.scalar.activation(out=tl[:], in_=log_tl[:], func=ACT.Exp)
         for k in range(len(CHUNKS)):
             transpose_chunk(0, k)
             quantise_chunk(0, k)
-        nc.scalar.activation(out=tl[:], in_=log_tl[:], func=ACT.Exp)
         nc.vector.tensor_scalar_mul(out=half_tl[:], in0=tl[:], scalar1=0.5)
         for b in range(2):
             nc.vector.tensor_copy(out=y[b][:, 1, :], in_=tl[:, 0:1].to_broadcast([P, HALF]))
@@ -275,84 +292,58 @@ def tile_recurrentsig_kernel(
                 out=spread[:], lhsT=ones[:], rhs=bias_rows[:, HALF * h : HALF * (h + 1)], start=True, stop=True
             )
             nc.scalar.copy(out=bias[:, HALF * h : HALF * (h + 1)], in_=spread[:])
-
+        for k in range(len(CHUNKS)):
+            transpose_chunk(1, k)
+            quantise_chunk(1, k)
+        if 0 in FED:
+            for q in range(4):
+                copy_sigs(0, q)
         from_inputs(0)
         product(0)
+        product(1)
         add_bias(0)
         displacement(0)
-        transpose_chunk(1, 0)
         level_one(0)
-        transpose_chunk(1, 1)
         level_two(0)
-        quantise_chunk(1, 0)
-        transpose_chunk(1, 2)
-        add_and_store(0, 0)
-        quantise_chunk(1, 1)
-        quantise_chunk(1, 2)
-        transpose_chunk(1, 3)
-        transpose_chunk(1, 4)
-        quantise_chunk(1, 3)
-        quantise_chunk(1, 4)
-        add_and_store(0, 1)
-        load_rows(3)
-        from_inputs(1)
-        product(1)
-        product(2)
-        add_bias(1)
-        displacement(1)
-        level_one(1)
-        level_two(1)
 
-        for i in range(1, len(UNITS)):
-            new_tile = PREPARED_DURING.get(i)
-            follower = i < LAST
-            if follower:
-                from_inputs(i + 1)
-            for early in PRODUCTS_BEFORE.get(i, ()):
-                product(early)
+        TILE_IN = {1: 2, 2: 3}
+        for i in range(len(UNITS)):
+            nxt = i + 1
+            new_tile = TILE_IN.get(i)
+            if nxt <= LAST:
+                from_inputs(nxt)
+            if i + 2 <= LAST:
+                product(i + 2)
             if new_tile:
-                for k in range(3):
+                for k in range(len(CHUNKS)):
                     transpose_chunk(new_tile, k)
-            if i in VIA_PSUM:
-                add_bias(i + 1)
-                displacement(i + 1)
-                planes_on_gpsimd(i + 1)
+            if nxt <= LAST and nxt in ON_GPSIMD:
+                add_bias(nxt)
+                displacement(nxt)
+                planes_on_gpsimd(nxt)
                 for q in range(4):
                     add_quarter(i, q)
-                    if i + 1 in VIA_PSUM:
-                        copy_sigs(i + 1, q)
-                if new_tile:
-                    quantise_chunk(new_tile, 0)
-                    transpose_chunk(new_tile, 3)
-                    quantise_chunk(new_tile, 1)
-                    transpose_chunk(new_tile, 4)
-                    quantise_chunk(new_tile, 2)
-                    quantise_chunk(new_tile, 3)
-                    quantise_chunk(new_tile, 4)
+                    if nxt in FED:
+                        copy_sigs(nxt, q)
+            elif nxt <= LAST:
+                add_bias(nxt)
+                add_quarter(i, 0)
+                displacement(nxt)
+                add_quarter(i, 1)
+                level_one(nxt)
+                add_quarter(i, 2)
+                level_two(nxt)
+                add_quarter(i, 3)
+                if nxt in FED:
+                    for q in range(4):
+                        copy_sigs(nxt, q)
             else:
-                add_and_store(i, 0)
-                if follower:
-                    add_bias(i + 1)
-                add_and_store(i, 1)
-                if new_tile:
-                    quantise_chunk(new_tile, 0)
-                    transpose_chunk(new_tile, 3)
-                if follower:
-                    displacement(i + 1)
-                if new_tile:
-                    quantise_chunk(new_tile, 1)
-                    transpose_chunk(new_tile, 4)
-                if follower:
-                    level_one(i + 1)
-                if new_tile:
-                    quantise_chunk(new_tile, 2)
-                if follower:
-                    level_two(i + 1)
-                if new_tile:
-                    quantise_chunk(new_tile, 3)
-                    quantise_chunk(new_tile, 4)
-            for later in PRODUCTS_AFTER.get(i, ()):
-                product(later)
-            if i + 1 == VIA_PSUM[0]:
-                for q in range(4):
-                    copy_sigs(i + 1, q)
+                add_quarter(i, 0)
+                add_quarter(i, 1)
+                for n0, nn in ((256, 128), (384, 64), (448, 64)):
+                    add_tail(i, n0, nn)
+            if new_tile:
+                for k in range(len(CHUNKS)):
+                    quantise_chunk(new_tile, k)
+            if i == 0:
+                load_rows(3)

@@ -28,8 +28,8 @@ WORD_LOADS = ((0, 3), (3, 7), (7, 11), (11, 13), (13, 14))
 UNITS = [(0, 0), (1, 0), (0, 1), (1, 1), (2, 0), (3, 0), (2, 1), (3, 1)]
 LAST = len(UNITS) - 1
 PREPARED_DURING = {1: 2, 2: 3}
-FED = (0, 4, 5, 6,)
-ON_GPSIMD = (1, 5, 6, 7,)
+FED = (0, 3, 4, 5, 6,)
+ON_GPSIMD = (1, 4, 5, 6, 7,)
 PRODUCTS_BEFORE = {1: (3,)}
 PRODUCTS_AFTER = {1: (4,), 2: (5,), 3: (6,), 4: (7,)}
 PARTS = (((0, 256),), ((256, 256),))

@@ -49,12 +49,12 @@ def tile_recurrentsig_kernel(
         ps_acc = ctx.enter_context(tc.psum_pool(name="ps_acc", bufs=3))
         ctx.enter_context(tc.manual_schedule())
 
-        u_scales = [keep.tile([P, PASSES - 1, HALF], U8, name="wscl%d" % h, align_bytes=64) for h in range(2)]
-        w_scales = keep.tile([P, 2 * HALF], U8, name="wscl_x", align_bytes=64)
-        words = [keep.tile([P, PASSES, 2 * HALF], U8, name="ww%d" % h, align_bytes=64) for h in range(2)]
+        u_scales = [keep.tile([P, PASSES - 1, HALF], U8, name="wscl%d" % h, align_bytes=256) for h in range(2)]
+        w_scales = keep.tile([P, 2 * HALF], U8, name="wscl_x", align_bytes=256)
+        words = [keep.tile([P, PASSES, 2 * HALF], U8, name="ww%d" % h, align_bytes=256) for h in range(2)]
         rows_in = [keep.tile([P, 512 * PASSES], BF16, name="mem%d" % m, align_bytes=64) for m in range(BATCH_TILES)]
-        codes = [keep.tile([P, PASSES * P], U32, name="codes%d" % m, align_bytes=64) for m in range(BATCH_TILES)]
-        act_scales = [keep.tile([P, PASSES * P], U8, name="ascl%d" % m, align_bytes=64) for m in range(BATCH_TILES)]
+        codes = [keep.tile([P, PASSES * P], U32, name="codes%d" % m, align_bytes=256) for m in range(BATCH_TILES)]
+        act_scales = [keep.tile([P, PASSES * P], U8, name="ascl%d" % m, align_bytes=256) for m in range(BATCH_TILES)]
         ident = keep.tile([P, P], F32, name="ident")
         ident_bf = keep.tile([P, P], BF16, name="identb")
         ones = keep.tile([P, P], BF16, name="ones")

@@ -52,7 +52,7 @@ def tile_recurrentsig_kernel(
         u_scales = [keep.tile([P, PASSES - 1, HALF], U8, name="wscl%d" % h, align_bytes=256) for h in range(2)]
         w_scales = keep.tile([P, 2 * HALF], U8, name="wscl_x", align_bytes=256)
         words = [keep.tile([P, PASSES, 2 * HALF], U8, name="ww%d" % h, align_bytes=256) for h in range(2)]
-        rows_in = [keep.tile([P, 512 * PASSES], BF16, name="mem%d" % m, align_bytes=64) for m in range(BATCH_TILES)]
+        rows_in = [keep.tile([P, 512 * PASSES], BF16, name="mem%d" % m, align_bytes=256) for m in range(BATCH_TILES)]
         codes = [keep.tile([P, PASSES * P], U32, name="codes%d" % m, align_bytes=256) for m in range(BATCH_TILES)]
         act_scales = [keep.tile([P, PASSES * P], U8, name="ascl%d" % m, align_bytes=256) for m in range(BATCH_TILES)]
         ident = keep.tile([P, P], F32, name="ident")
@@ -117,7 +117,7 @@ def tile_recurrentsig_kernel(
         def transpose_chunk(m, k):
             g0, n = CHUNKS[k]
             row_words = rows_in[m][:].bitcast(F32)
-            grouped = stage.tile([P, 2048], BF16, name="gs", align_bytes=64)
+            grouped = stage.tile([P, 2048], BF16, name="gs", align_bytes=256)
             grouped_words = grouped[:].bitcast(F32).rearrange("p (g r u) -> p g r u", g=4, u=2)
             for b0 in range(0, n, 2):
                 nb = min(2, n - b0)
@@ -176,7 +176,7 @@ def tile_recurrentsig_kernel(
 
         def add_bias(i):
             m, h = UNITS[i]
-            raw = rawp.tile([P, HALF], F32, name="rt")
+            raw = rawp.tile([P, HALF], F32, name="rt", align_bytes=256)
             raws[i] = raw
             nc.vector.tensor_tensor(out=raw[:], in0=products[i][:], in1=bias[:, HALF * h : HALF * (h + 1)], op=ALU.add)
             c0 = 1024 * SIG + HALF * h
@@ -227,7 +227,7 @@ def tile_recurrentsig_kernel(
 
         def add_tail(i, n0, nn):
             m, h = UNITS[i]
-            new_sigs = outp.tile([P, 128, 2, SIG], F32, name="ot")
+            new_sigs = outp.tile([P, 128, 2, SIG], F32, name="ot", align_bytes=256)
             c0 = SIG * (HALF * h + n0)
             nc.vector.tensor_tensor(
                 out=new_sigs[:, 0 : nn // 2, :, :].rearrange("p m t c -> p m c t"),
@@ -243,7 +243,7 @@ def tile_recurrentsig_kernel(
         def add_quarter(i, q):
             m, h = UNITS[i]
             if q % 2 == 0:
-                new_sigs = outp.tile([P, 128, 2, SIG], F32, name="ot")
+                new_sigs = outp.tile([P, 128, 2, SIG], F32, name="ot", align_bytes=256)
                 out_tiles[i] = new_sigs
             new_sigs = out_tiles[i]
             m0 = 64 * (q % 2)
@@ -264,7 +264,7 @@ def tile_recurrentsig_kernel(
         def add_and_store(i, j):
             m, h = UNITS[i]
             for n0, nn in (PARTS_OF_LAST if i == LAST else PARTS)[j]:
-                new_sigs = outp.tile([P, 128, 2, SIG], F32, name="ot")
+                new_sigs = outp.tile([P, 128, 2, SIG], F32, name="ot", align_bytes=256)
                 c0 = SIG * (HALF * h + n0)
                 nc.vector.tensor_tensor(
                     out=new_sigs[:, 0 : nn // 2, :, :].rearrange("p m t c -> p m c t"),

@@ -66,6 +66,18 @@ def tile_recurrentsig_kernel(
         y = [keep.tile([P, SIG, HALF], F32, name="ypl%d" % b) for b in range(2)]
         aux = [keep.tile([P, 4, HALF], F32, name="upl%d" % b) for b in range(2)]
 
+        y_last = y[LAST % 2][:].rearrange("p c n -> p (c n)").rearrange("p (a c n) -> p a c n", a=2, c=SIG)
+
+        def plane(i, c, c0=0, w=HALF):
+            if i == LAST:
+                return y_last[:, c0 // 256, c, c0 % 256 : c0 % 256 + w]
+            return y[i % 2][:, c, c0 : c0 + w]
+
+        def planes(i, n0, nn):
+            if i == LAST:
+                return y_last[:, n0 // 256, :, n0 % 256 : n0 % 256 + nn]
+            return y[i % 2][:, :, n0 : n0 + nn]
+
         make_identity(nc, ident[:])
         make_identity(nc, ident_bf[:])
         nc.vector.memset(bias_rows[:], 0.0)
@@ -144,7 +156,7 @@ def tile_recurrentsig_kernel(
         def product(i):
             m, h = UNITS[i]
             acc = ps_acc.tile([P, HALF], F32, name="acc")
-            products[i] = acc
+            products[(i, 0)] = acc
             for g in range(PASSES):
                 nc.tensor.matmul_mx(
                     out=acc[:],
@@ -155,6 +167,25 @@ def tile_recurrentsig_kernel(
                     start=(g == 0),
                     stop=(g == PASSES - 1),
                 )
+
+        def narrow_product(i, c0):
+            m, h = UNITS[i]
+            acc = ps_acc.tile([P, HALF], F32, name="acc")
+            products[(i, c0)] = acc
+            for n0 in (0, P):
+                c = c0 + n0
+                for g in range(PASSES):
+                    nc.tensor.matmul_mx(
+                        out=acc[:, n0 : n0 + P],
+                        lhsT=codes[m][:, P * g : P * (g + 1)].bitcast(FP8X4),
+                        lhsT_scale=act_scales[m][:, P * g : P * (g + 1)],
+                        rhs=words[h][:, g, 2 * c : 2 * (c + P)].bitcast(FP4X4),
+                        rhs_scale=(
+                            w_scales[:, HALF * h + c : HALF * h + c + P] if g == 0 else u_scales[h][:, g - 1, c : c + P]
+                        ),
+                        start=(g == 0),
+                        stop=(g == PASSES - 1),
+                    )
 
         def old_sigs(i):
             m, h = UNITS[i]
@@ -170,25 +201,37 @@ def tile_recurrentsig_kernel(
             nc.scalar.activation(
                 out=aux[b][:, 1, :], in_=old_sigs(i)[:, :, 1], func=ACT.Identity, bias=half_tl[:, 0:1], scale=1.0
             )
-            nc.scalar.mul(out=y[b][:, 5, :], in_=aux[b][:, 1, :], mul=tl[:, 0:1])
+            if i == LAST:
+                for c0 in (0, 256):
+                    nc.scalar.mul(out=plane(i, 5, c0, 256), in_=aux[b][:, 1, c0 : c0 + 256], mul=tl[:, 0:1])
+                    nc.scalar.activation(
+                        out=plane(i, 1, c0, 256), in_=aux[b][:, 1, c0 : c0 + 256], func=ACT.Identity, bias=tl[:, 0:1], scale=0.0
+                    )
+            else:
+                nc.scalar.mul(out=y[b][:, 5, :], in_=aux[b][:, 1, :], mul=tl[:, 0:1])
 
         raws = {}
 
-        def add_bias(i):
+        def add_bias(i, c0=0, w=HALF):
             m, h = UNITS[i]
-            raw = rawp.tile([P, HALF], F32, name="rt", align_bytes=256)
-            raws[i] = raw
-            nc.vector.tensor_tensor(out=raw[:], in0=products[i][:], in1=bias[:, HALF * h : HALF * (h + 1)], op=ALU.add)
-            c0 = 1024 * SIG + HALF * h
-            nc.sync.dma_start(out=out[P * m : P * m + P, c0 : c0 + HALF], in_=raw[:])
-
-        def displacement(i):
-            m, h = UNITS[i]
+            if c0 == 0:
+                raw = rawp.tile([P, HALF], F32, name="rt", align_bytes=256)
+                raws[i] = raw
+            raw = raws[i]
             nc.vector.tensor_tensor(
-                out=y[i % 2][:, 0, :],
-                in0=raws[i][:],
-                in1=rows_in[m][:, STATE_COL + HALF * h : STATE_COL + HALF * (h + 1)],
-                op=ALU.subtract,
+                out=raw[:, c0 : c0 + w],
+                in0=products[(i, c0)][:, 0:w],
+                in1=bias[:, HALF * h + c0 : HALF * h + c0 + w],
+                op=ALU.add,
+            )
+            o0 = 1024 * SIG + HALF * h + c0
+            nc.sync.dma_start(out=out[P * m : P * m + P, o0 : o0 + w], in_=raw[:, c0 : c0 + w])
+
+        def displacement(i, c0=0, w=HALF):
+            m, h = UNITS[i]
+            s0 = STATE_COL + HALF * h + c0
+            nc.vector.tensor_tensor(
+                out=plane(i, 0, c0, w), in0=raws[i][:, c0 : c0 + w], in1=rows_in[m][:, s0 : s0 + w], op=ALU.subtract
             )
 
         def level_one(i):
@@ -203,13 +246,15 @@ def tile_recurrentsig_kernel(
             for w in range(2):
                 nc.vector.tensor_tensor(out=y[b][:, 2 + 2 * w, :], in0=y[b][:, 0, :], in1=aux[b][:, w, :], op=ALU.mult)
 
-        def planes_on_gpsimd(i):
+        def planes_on_gpsimd(i, c0=0, w=HALF):
             b = i % 2
-            nc.gpsimd.tensor_tensor(out=aux[b][:, 0, :], in0=y[b][:, 0, :], in1=aux[b][:, 2, :], op=ALU.add)
-            nc.scalar.mul(out=y[b][:, 3, :], in_=aux[b][:, 0, :], mul=half_tl[:, 0:1])
-            nc.gpsimd.tensor_tensor(out=aux[b][:, 3, :], in0=y[b][:, 0, :], in1=aux[b][:, 0, :], op=ALU.mult)
-            nc.scalar.mul(out=y[b][:, 2, :], in_=aux[b][:, 3, :], mul=0.5)
-            nc.gpsimd.tensor_tensor(out=y[b][:, 4, :], in0=y[b][:, 0, :], in1=aux[b][:, 1, :], op=ALU.mult)
+            cols = slice(c0, c0 + w)
+            d = plane(i, 0, c0, w)
+            nc.gpsimd.tensor_tensor(out=aux[b][:, 0, cols], in0=d, in1=aux[b][:, 2, cols], op=ALU.add)
+            nc.scalar.mul(out=plane(i, 3, c0, w), in_=aux[b][:, 0, cols], mul=half_tl[:, 0:1])
+            nc.gpsimd.tensor_tensor(out=aux[b][:, 3, cols], in0=d, in1=aux[b][:, 0, cols], op=ALU.mult)
+            nc.scalar.mul(out=plane(i, 2, c0, w), in_=aux[b][:, 3, cols], mul=0.5)
+            nc.gpsimd.tensor_tensor(out=plane(i, 4, c0, w), in0=d, in1=aux[b][:, 1, cols], op=ALU.mult)
 
         sig_banks = {}
 
@@ -225,19 +270,23 @@ def tile_recurrentsig_kernel(
 
         out_tiles = {}
 
-        def add_tail(i, n0, nn):
+        def add_tail(i, n0, nn, engine):
             m, h = UNITS[i]
-            new_sigs = outp.tile([P, 128, 2, SIG], F32, name="ot", align_bytes=256)
+            if n0 == 256:
+                new_sigs = outp.tile([P, 128, 2, SIG], F32, name="ot", align_bytes=256)
+                out_tiles[i] = new_sigs
+            new_sigs = out_tiles[i]
+            m0 = (n0 - 256) // 2
             c0 = SIG * (HALF * h + n0)
-            nc.vector.tensor_tensor(
-                out=new_sigs[:, 0 : nn // 2, :, :].rearrange("p m t c -> p m c t"),
+            engine.tensor_tensor(
+                out=new_sigs[:, m0 : m0 + nn // 2, :, :].rearrange("p m t c -> p m c t"),
                 in0=rows_in[m][:, X_COLS + c0 : X_COLS + c0 + SIG * nn].rearrange("p (m t c) -> p m c t", t=2, c=SIG),
-                in1=y[i % 2][:, :, n0 : n0 + nn].rearrange("p c (m t) -> p m c t", t=2),
+                in1=planes(i, n0, nn).rearrange("p c (m t) -> p m c t", t=2),
                 op=ALU.add,
             )
             nc.sync.dma_start(
                 out=out[P * m : P * m + P, c0 : c0 + SIG * nn],
-                in_=new_sigs[:, 0 : nn // 2, :, :].rearrange("p m t c -> p (m t c)"),
+                in_=new_sigs[:, m0 : m0 + nn // 2, :, :].rearrange("p m t c -> p (m t c)"),
             )
 
         def add_quarter(i, q):
@@ -248,11 +297,11 @@ def tile_recurrentsig_kernel(
             new_sigs = out_tiles[i]
             m0 = 64 * (q % 2)
             s0 = X_COLS + SIG * (HALF * h + 128 * q)
-            old = sig_banks[(i, q)][:, 0:768] if i in FED else rows_in[m][:, s0 : s0 + 768]
+            old = sig_banks[(i, q)][:, 0:768] if (i, q) in sig_banks else rows_in[m][:, s0 : s0 + 768]
             nc.vector.tensor_tensor(
                 out=new_sigs[:, m0 : m0 + 64, :, :].rearrange("p m t c -> p m c t"),
                 in0=old.rearrange("p (m t c) -> p m c t", t=2, c=SIG),
-                in1=y[i % 2][:, :, 128 * q : 128 * (q + 1)].rearrange("p c (m t) -> p m c t", t=2),
+                in1=planes(i, 128 * q, 128).rearrange("p c (m t) -> p m c t", t=2),
                 op=ALU.add,
             )
             if q % 2 == 1:
@@ -312,12 +361,26 @@ def tile_recurrentsig_kernel(
             new_tile = TILE_IN.get(i)
             if nxt <= LAST:
                 from_inputs(nxt)
-            if i + 2 <= LAST:
-                product(i + 2)
             if new_tile:
-                for k in range(len(CHUNKS)):
+                transpose_chunk(new_tile, 0)
+                transpose_chunk(new_tile, 1)
+            if i + 2 < LAST:
+                product(i + 2)
+            if i + 2 == LAST:
+                narrow_product(LAST, 0)
+            if new_tile:
+                for k in range(2, len(CHUNKS)):
                     transpose_chunk(new_tile, k)
-            if nxt <= LAST and nxt in ON_GPSIMD:
+            if nxt == LAST:
+                for c0 in (0, 256):
+                    add_bias(nxt, c0, 256)
+                    displacement(nxt, c0, 256)
+                    planes_on_gpsimd(nxt, c0, 256)
+                    for q in (c0 // 128, c0 // 128 + 1):
+                        add_quarter(i, q)
+                        if q < 2:
+                            copy_sigs(nxt, q)
+            elif nxt in ON_GPSIMD:
                 add_bias(nxt)
                 displacement(nxt)
                 planes_on_gpsimd(nxt)
@@ -325,7 +388,9 @@ def tile_recurrentsig_kernel(
                     add_quarter(i, q)
                     if nxt in FED:
                         copy_sigs(nxt, q)
-            elif nxt <= LAST:
+                    if i + 2 == LAST and q == 1:
+                        narrow_product(LAST, 256)
+            elif nxt < LAST:
                 add_bias(nxt)
                 add_quarter(i, 0)
                 displacement(nxt)
@@ -341,7 +406,7 @@ def tile_recurrentsig_kernel(
                 add_quarter(i, 0)
                 add_quarter(i, 1)
                 for n0, nn in ((256, 128), (384, 64), (448, 64)):
-                    add_tail(i, n0, nn)
+                    add_tail(i, n0, nn, nc.vector)
             if new_tile:
                 for k in range(len(CHUNKS)):
                     quantise_chunk(new_tile, k)

@@ -243,8 +243,9 @@ def tile_recurrentsig_kernel(
 
         def level_two(i):
             b = i % 2
-            for w in range(2):
-                nc.vector.tensor_tensor(out=y[b][:, 2 + 2 * w, :], in0=y[b][:, 0, :], in1=aux[b][:, w, :], op=ALU.mult)
+            nc.vector.tensor_tensor(
+                out=y[b][:, 2:5:2, :], in0=y[b][:, 0:1, :].to_broadcast([P, 2, HALF]), in1=aux[b][:, 0:2, :], op=ALU.mult
+            )
 
         def planes_on_gpsimd(i, c0=0, w=HALF):
             b = i % 2
@@ -287,6 +288,20 @@ def tile_recurrentsig_kernel(
             nc.sync.dma_start(
                 out=out[P * m : P * m + P, c0 : c0 + SIG * nn],
                 in_=new_sigs[:, m0 : m0 + nn // 2, :, :].rearrange("p m t c -> p (m t c)"),
+            )
+
+        def add_half(i, j):
+            m, h = UNITS[i]
+            new_sigs = outp.tile([P, 128, 2, SIG], F32, name="ot", align_bytes=256)
+            c0 = SIG * (HALF * h + 256 * j)
+            nc.vector.tensor_tensor(
+                out=new_sigs[:].rearrange("p m t c -> p m c t"),
+                in0=rows_in[m][:, X_COLS + c0 : X_COLS + c0 + SIG * 256].rearrange("p (m t c) -> p m c t", t=2, c=SIG),
+                in1=planes(i, 256 * j, 256).rearrange("p c (m t) -> p m c t", t=2),
+                op=ALU.add,
+            )
+            nc.sync.dma_start(
+                out=out[P * m : P * m + P, c0 : c0 + SIG * 256], in_=new_sigs[:].rearrange("p m t c -> p (m t c)")
             )
 
         def add_quarter(i, q):
@@ -392,13 +407,12 @@ def tile_recurrentsig_kernel(
                         narrow_product(LAST, 256)
             elif nxt < LAST:
                 add_bias(nxt)
-                add_quarter(i, 0)
+                add_half(i, 0)
                 displacement(nxt)
-                add_quarter(i, 1)
+                add_half(i, 1)
                 level_one(nxt)
-                add_quarter(i, 2)
+                quantise_chunk(new_tile, 0)
                 level_two(nxt)
-                add_quarter(i, 3)
                 if nxt in FED:
                     for q in range(4):
                         copy_sigs(nxt, q)
@@ -408,7 +422,7 @@ def tile_recurrentsig_kernel(
                 for n0, nn in ((256, 128), (384, 64), (448, 64)):
                     add_tail(i, n0, nn, nc.vector)
             if new_tile:
-                for k in range(len(CHUNKS)):
+                for k in range(1, len(CHUNKS)):
                     quantise_chunk(new_tile, k)
             if i == 0:
                 load_rows(3)

@@ -60,7 +60,8 @@ def tile_recurrentsig_kernel(
         ones = keep.tile([P, P], BF16, name="ones")
         bias_rows = keep.tile([P, 2 * HALF], BF16, name="zb")
         bias = keep.tile([P, 2 * HALF], F32, name="beta")
-        log_tl = keep.tile([P, 1], BF16, name="ltb")
+        log_row = keep.tile([P, 2], BF16, name="ltb")
+        warm = keep.tile([P, 1], F32, name="warm")
         tl = keep.tile([P, 1], F32, name="tl")
         half_tl = keep.tile([P, 1], F32, name="htl")
         y = [keep.tile([P, SIG, HALF], F32, name="ypl%d" % b) for b in range(2)]
@@ -80,12 +81,14 @@ def tile_recurrentsig_kernel(
 
         make_identity(nc, ident[:])
         make_identity(nc, ident_bf[:])
+        nc.vector.memset(warm[:], 0.0)
+        nc.vector.memset(log_row[:], 0.0)
         nc.vector.memset(bias_rows[:], 0.0)
         nc.vector.memset(ones[:], 1.0)
         nc.vector.memset(w_scales[:].bitcast(I32), 0)
         for h in range(2):
             nc.vector.memset(u_scales[h][:].rearrange("p g n -> p (g n)").bitcast(I32), 0)
-        nc.scalar.dma_start(out=log_tl[:], in_=log_timelapse.partition_broadcast(P))
+        nc.scalar.dma_start(out=log_row[0:1, 0:1], in_=log_timelapse.rearrange("(o n) -> o n", o=1))
         nc.scalar.dma_start(out=bias_rows[0:1, :], in_=W_b.rearrange("(o n) -> o n", o=1))
         nc.scalar.dma_start(out=bias_rows[1:2, :], in_=U_b.rearrange("(o n) -> o n", o=1))
 
@@ -343,10 +346,13 @@ def tile_recurrentsig_kernel(
                     in_=new_sigs[:, 0 : nn // 2, :, :].rearrange("p m t c -> p (m t c)"),
                 )
 
-        nc.scalar.activation(out=tl[:], in_=log_tl[:], func=ACT.Exp)
+        nc.scalar.activation(out=warm[:], in_=warm[:], func=ACT.Exp)
         for k in range(len(CHUNKS)):
             transpose_chunk(0, k)
             quantise_chunk(0, k)
+        spread = ps_acc.tile([P, HALF], F32, name="acc")
+        nc.tensor.matmul(out=spread[:, 0:2], lhsT=ones[:], rhs=log_row[:], start=True, stop=True)
+        nc.scalar.activation(out=tl[:], in_=spread[:, 0:1], func=ACT.Exp)
         nc.vector.tensor_scalar_mul(out=half_tl[:], in0=tl[:], scalar1=0.5)
         for b in range(2):
             nc.vector.tensor_copy(out=y[b][:, 1, :], in_=tl[:, 0:1].to_broadcast([P, HALF]))

@@ -322,10 +322,13 @@ def tile_recurrentsig_kernel(
                 in1=planes(i, 128 * q, 128).rearrange("p c (m t) -> p m c t", t=2),
                 op=ALU.add,
             )
-            if q % 2 == 1:
-                c0 = SIG * (HALF * h + 128 * (q - 1))
+            if i >= LAST - 1 or q % 2 == 1:
+                first = q if i >= LAST - 1 else q - 1
+                c0 = SIG * (HALF * h + 128 * first)
+                done = new_sigs[:, 64 * (first % 2) : m0 + 64, :, :]
                 nc.sync.dma_start(
-                    out=out[P * m : P * m + P, c0 : c0 + SIG * 256], in_=new_sigs[:].rearrange("p m t c -> p (m t c)")
+                    out=out[P * m : P * m + P, c0 : c0 + SIG * 128 * (q - first + 1)],
+                    in_=done.rearrange("p m t c -> p (m t c)"),
                 )
 
         def add_and_store(i, j):

@@ -215,27 +215,31 @@ def tile_recurrentsig_kernel(
 
         raws = {}
 
-        def add_bias(i, c0=0, w=HALF):
+        def add_bias(i, c0=0, w=HALF, pieces=1):
             m, h = UNITS[i]
             if c0 == 0:
                 raw = rawp.tile([P, HALF], F32, name="rt", align_bytes=256)
                 raws[i] = raw
             raw = raws[i]
-            nc.vector.tensor_tensor(
-                out=raw[:, c0 : c0 + w],
-                in0=products[(i, c0)][:, 0:w],
-                in1=bias[:, HALF * h + c0 : HALF * h + c0 + w],
-                op=ALU.add,
-            )
+            for p0 in range(0, w, w // pieces):
+                piece = slice(c0 + p0, c0 + p0 + w // pieces)
+                nc.vector.tensor_tensor(
+                    out=raw[:, piece],
+                    in0=products[(i, c0)][:, p0 : p0 + w // pieces],
+                    in1=bias[:, HALF * h + piece.start : HALF * h + piece.stop],
+                    op=ALU.add,
+                )
             o0 = 1024 * SIG + HALF * h + c0
             nc.sync.dma_start(out=out[P * m : P * m + P, o0 : o0 + w], in_=raw[:, c0 : c0 + w])
 
-        def displacement(i, c0=0, w=HALF):
+        def displacement(i, c0=0, w=HALF, pieces=1):
             m, h = UNITS[i]
-            s0 = STATE_COL + HALF * h + c0
-            nc.vector.tensor_tensor(
-                out=plane(i, 0, c0, w), in0=raws[i][:, c0 : c0 + w], in1=rows_in[m][:, s0 : s0 + w], op=ALU.subtract
-            )
+            for p0 in range(c0, c0 + w, w // pieces):
+                wp = w // pieces
+                s0 = STATE_COL + HALF * h + p0
+                nc.vector.tensor_tensor(
+                    out=plane(i, 0, p0, wp), in0=raws[i][:, p0 : p0 + wp], in1=rows_in[m][:, s0 : s0 + wp], op=ALU.subtract
+                )
 
         def level_one(i):
             b = i % 2
@@ -374,8 +378,8 @@ def tile_recurrentsig_kernel(
         from_inputs(0)
         product(0)
         product(1)
-        add_bias(0)
-        displacement(0)
+        add_bias(0, pieces=2)
+        displacement(0, pieces=2)
         level_one(0)
         level_two(0)
 
@@ -398,15 +402,16 @@ def tile_recurrentsig_kernel(
             if nxt == LAST:
                 for c0 in (0, 256):
                     add_bias(nxt, c0, 256)
+                    add_quarter(i, c0 // 128)
                     displacement(nxt, c0, 256)
                     planes_on_gpsimd(nxt, c0, 256)
-                    for q in (c0 // 128, c0 // 128 + 1):
-                        add_quarter(i, q)
-                        if q < 2:
+                    add_quarter(i, c0 // 128 + 1)
+                    if c0 == 0:
+                        for q in range(2):
                             copy_sigs(nxt, q)
             elif nxt in ON_GPSIMD:
-                add_bias(nxt)
-                displacement(nxt)
+                add_bias(nxt, pieces=2)
+                displacement(nxt, pieces=2)
                 planes_on_gpsimd(nxt)
                 for q in range(4):
                     add_quarter(i, q)

@@ -326,8 +326,8 @@ def tile_recurrentsig_kernel(
                 in1=planes(i, 128 * q, 128).rearrange("p c (m t) -> p m c t", t=2),
                 op=ALU.add,
             )
-            if i >= LAST - 1 or q % 2 == 1:
-                first = q if i >= LAST - 1 else q - 1
+            if i >= LAST - 2 or q % 2 == 1:
+                first = q if i >= LAST - 2 else q - 1
                 c0 = SIG * (HALF * h + 128 * first)
                 done = new_sigs[:, 64 * (first % 2) : m0 + 64, :, :]
                 nc.sync.dma_start(

from contextlib import ExitStack

import concourse.mybir as mybir
from concourse.masks import make_identity

FLOPS = 2 * 512 * 7680 * 1024

F32 = mybir.dt.float32
BF16 = mybir.dt.bfloat16
U8 = mybir.dt.uint8
U32 = mybir.dt.uint32
I32 = mybir.dt.int32
FP8X4 = mybir.dt.float8_e4m3fn_x4
FP4X4 = mybir.dt.float4_e2m1fn_x4
ALU = mybir.AluOpType
ACT = mybir.ActivationFunctionType

P = 128
BATCH_TILES = 4
PASSES = 15
HALF = 512
SIG = 6
X_COLS = 512
STATE_COL = X_COLS + 1024 * SIG
CHUNKS = [(0, 4), (4, 4), (8, 4), (12, 2), (14, 1)]
SIG_LOADS = ((0, 1536), (1536, 3584), (3584, 5632), (5632, 6144))
WORD_LOADS = ((0, 3), (3, 7), (7, 11), (11, 13), (13, 14))
UNITS = [(0, 0), (1, 0), (0, 1), (1, 1), (2, 0), (3, 0), (2, 1), (3, 1)]
LAST = len(UNITS) - 1
PREPARED_DURING = {1: 2, 2: 3}
FED = (0, 3, 4, 5, 6,)
ON_GPSIMD = (1, 4, 5, 6, 7,)
PRODUCTS_BEFORE = {1: (3,)}
PRODUCTS_AFTER = {1: (4,), 2: (5,), 3: (6,), 4: (7,)}
PARTS = (((0, 256),), ((256, 256),))
PARTS_OF_LAST = (((0, 256),), ((256, 128), (384, 64), (448, 64)))


def tile_recurrentsig_kernel(
    tc, x, prev_sigs, prev_states, W_w_words, W_w_scales, W_b, U_w_words, U_w_scales, U_b, log_timelapse, out
):
    nc = tc.nc
    with ExitStack() as ctx:
        keep = ctx.enter_context(tc.tile_pool(name="keep", bufs=1))
        stage = ctx.enter_context(tc.tile_pool(name="stage", bufs=3))
        outp = ctx.enter_context(tc.tile_pool(name="outp", bufs=4))
        rawp = ctx.enter_context(tc.tile_pool(name="rawp", bufs=3))
        ps_tr = ctx.enter_context(tc.psum_pool(name="ps_tr", bufs=5))
        ps_acc = ctx.enter_context(tc.psum_pool(name="ps_acc", bufs=3))
        ctx.enter_context(tc.manual_schedule())

        u_scales = [keep.tile([P, PASSES - 1, HALF], U8, name="wscl%d" % h, align_bytes=256) for h in range(2)]
        w_scales = keep.tile([P, 2 * HALF], U8, name="wscl_x", align_bytes=256)
        words = [keep.tile([P, PASSES, 2 * HALF], U8, name="ww%d" % h, align_bytes=256) for h in range(2)]
        rows_in = [keep.tile([P, 512 * PASSES], BF16, name="mem%d" % m, align_bytes=256) for m in range(BATCH_TILES)]
        codes = [keep.tile([P, PASSES * P], U32, name="codes%d" % m, align_bytes=256) for m in range(BATCH_TILES)]
        act_scales = [keep.tile([P, PASSES * P], U8, name="ascl%d" % m, align_bytes=256) for m in range(BATCH_TILES)]
        ident = keep.tile([P, P], F32, name="ident")
        ident_bf = keep.tile([P, P], BF16, name="identb")
        ones = keep.tile([P, P], BF16, name="ones")
        bias_rows = keep.tile([P, 2 * HALF], BF16, name="zb")
        bias = keep.tile([P, 2 * HALF], F32, name="beta")
        log_row = keep.tile([P, 2], BF16, name="ltb")
        warm = keep.tile([P, 1], F32, name="warm")
        tl = keep.tile([P, 1], F32, name="tl")
        half_tl = keep.tile([P, 1], F32, name="htl")
        y = [keep.tile([P, SIG, HALF], F32, name="ypl%d" % b) for b in range(2)]
        aux = [keep.tile([P, 4, HALF], F32, name="upl%d" % b) for b in range(2)]

        y_last = y[LAST % 2][:].rearrange("p c n -> p (c n)").rearrange("p (a c n) -> p a c n", a=2, c=SIG)

        def plane(i, c, c0=0, w=HALF):
            if i == LAST:
                return y_last[:, c0 // 256, c, c0 % 256 : c0 % 256 + w]
            return y[i % 2][:, c, c0 : c0 + w]

        def planes(i, n0, nn):
            if i == LAST:
                return y_last[:, n0 // 256, :, n0 % 256 : n0 % 256 + nn]
            return y[i % 2][:, :, n0 : n0 + nn]

        make_identity(nc, ident[:])
        make_identity(nc, ident_bf[:])
        nc.vector.memset(warm[:], 0.0)
        nc.vector.memset(log_row[:], 0.0)
        nc.vector.memset(bias_rows[:], 0.0)
        nc.vector.memset(ones[:], 1.0)
        nc.vector.memset(w_scales[:].bitcast(I32), 0)
        for h in range(2):
            nc.vector.memset(u_scales[h][:].rearrange("p g n -> p (g n)").bitcast(I32), 0)
        nc.scalar.dma_start(out=log_row[0:1, 0:1], in_=log_timelapse.rearrange("(o n) -> o n", o=1))
        nc.scalar.dma_start(out=bias_rows[0:1, :], in_=W_b.rearrange("(o n) -> o n", o=1))
        nc.scalar.dma_start(out=bias_rows[1:2, :], in_=U_b.rearrange("(o n) -> o n", o=1))

        def load_rows(m):
            rows = slice(P * m, P * m + P)
            nc.sync.dma_start(out=rows_in[m][:, 0:X_COLS], in_=x[rows, :])
            for c0, c1 in SIG_LOADS:
                nc.sync.dma_start(out=rows_in[m][:, X_COLS + c0 : X_COLS + c1], in_=prev_sigs[rows, c0:c1])
            nc.sync.dma_start(out=rows_in[m][:, STATE_COL : 512 * PASSES], in_=prev_states[rows, :])

        def load_scales(h):
            cols = slice(HALF * h, HALF * h + HALF)
            for r in range(4):
                nc.sync.dma_start(
                    out=u_scales[h][r : P : 32, :, :].bitcast(I32),
                    in_=U_w_scales[:, r : 16 : 4, cols].rearrange("g q n -> q g n").bitcast(I32),
                )
            if h == 0:
                for r in range(4):
                    nc.sync.dma_start(out=w_scales[r:P:32, :].bitcast(I32), in_=W_w_scales[0, r:16:4, :].bitcast(I32))

        def load_words(h):
            cols = slice(2 * HALF * h, 2 * HALF * h + 2 * HALF)
            nc.sync.dma_start(out=words[h][:, 0, :].bitcast(I32), in_=W_w_words[0, :, cols].bitcast(I32))
            for g0, g1 in WORD_LOADS:
                nc.sync.dma_start(
                    out=words[h][:, 1 + g0 : 1 + g1, :].bitcast(I32),
                    in_=U_w_words[g0:g1, :, cols].rearrange("g p n -> p g n").bitcast(I32),
                )

        load_rows(0)
        load_rows(1)
        load_scales(0)
        load_words(0)
        load_scales(1)
        load_words(1)
        load_rows(2)

        regrouped = {}

        def transpose_chunk(m, k):
            g0, n = CHUNKS[k]
            row_words = rows_in[m][:].bitcast(F32)
            grouped = stage.tile([P, 2048], BF16, name="gs", align_bytes=256)
            grouped_words = grouped[:].bitcast(F32).rearrange("p (g r u) -> p g r u", g=4, u=2)
            for b0 in range(0, n, 2):
                nb = min(2, n - b0)
                bank = ps_tr.tile([P, 2, 2, P], F32, name="tr", tag="tr")
                for gg in range(nb):
                    g = g0 + b0 + gg
                    for u in range(2):
                        nc.tensor.transpose(bank[:, gg, u, :], row_words[:, 256 * g + u : 256 * (g + 1) : 2], ident[:])
                nc.scalar.copy(
                    out=grouped_words[:, b0 : b0 + nb, :, :], in_=bank[:, 0:nb, :, :].rearrange("p g u r -> p g r u")
                )
            regrouped[(m, k)] = grouped

        def quantise_chunk(m, k):
            g0, n = CHUNKS[k]
            nc.vector.quantize_mx(
                out=codes[m][:, P * g0 : P * (g0 + n)].bitcast(FP8X4),
                scales=act_scales[m][:, P * g0 : P * (g0 + n)],
                in_=regrouped[(m, k)][:, 0 : 512 * n],
            )

        products = {}

        def product(i):
            m, h = UNITS[i]
            acc = ps_acc.tile([P, HALF], F32, name="acc")
            products[(i, 0)] = acc
            for g in range(PASSES):
                nc.tensor.matmul_mx(
                    out=acc[:],
                    lhsT=codes[m][:, P * g : P * (g + 1)].bitcast(FP8X4),
                    lhsT_scale=act_scales[m][:, P * g : P * (g + 1)],
                    rhs=words[h][:, g, :].bitcast(FP4X4),
                    rhs_scale=(w_scales[:, HALF * h : HALF * (h + 1)] if g == 0 else u_scales[h][:, g - 1, :]),
                    start=(g == 0),
                    stop=(g == PASSES - 1),
                )

        def narrow_product(i, c0):
            m, h = UNITS[i]
            acc = ps_acc.tile([P, HALF], F32, name="acc")
            products[(i, c0)] = acc
            for n0 in (0, P):
                c = c0 + n0
                for g in range(PASSES):
                    nc.tensor.matmul_mx(
                        out=acc[:, n0 : n0 + P],
                        lhsT=codes[m][:, P * g : P * (g + 1)].bitcast(FP8X4),
                        lhsT_scale=act_scales[m][:, P * g : P * (g + 1)],
                        rhs=words[h][:, g, 2 * c : 2 * (c + P)].bitcast(FP4X4),
                        rhs_scale=(
                            w_scales[:, HALF * h + c : HALF * h + c + P] if g == 0 else u_scales[h][:, g - 1, c : c + P]
                        ),
                        start=(g == 0),
                        stop=(g == PASSES - 1),
                    )

        def old_sigs(i):
            m, h = UNITS[i]
            c0 = X_COLS + SIG * HALF * h
            return rows_in[m][:, c0 : c0 + SIG * HALF].rearrange("p (n c) -> p n c", c=SIG)

        def from_inputs(i):
            b = i % 2
            if i in ON_GPSIMD:
                nc.scalar.mul(out=aux[b][:, 2, :], in_=old_sigs(i)[:, :, 0], mul=2.0)
            else:
                nc.scalar.copy(out=aux[b][:, 2, :], in_=old_sigs(i)[:, :, 0])
            nc.scalar.activation(
                out=aux[b][:, 1, :], in_=old_sigs(i)[:, :, 1], func=ACT.Identity, bias=half_tl[:, 0:1], scale=1.0
            )
            if i == LAST:
                for c0 in (0, 256):
                    nc.scalar.mul(out=plane(i, 5, c0, 256), in_=aux[b][:, 1, c0 : c0 + 256], mul=tl[:, 0:1])
                    nc.scalar.activation(
                        out=plane(i, 1, c0, 256), in_=aux[b][:, 1, c0 : c0 + 256], func=ACT.Identity, bias=tl[:, 0:1], scale=0.0
                    )
            else:
                nc.scalar.mul(out=y[b][:, 5, :], in_=aux[b][:, 1, :], mul=tl[:, 0:1])

        raws = {}

        def add_bias(i, c0=0, w=HALF, pieces=1):
            m, h = UNITS[i]
            if c0 == 0:
                raw = rawp.tile([P, HALF], F32, name="rt", align_bytes=256)
                raws[i] = raw
            raw = raws[i]
            for p0 in range(0, w, w // pieces):
                piece = slice(c0 + p0, c0 + p0 + w // pieces)
                nc.vector.tensor_tensor(
                    out=raw[:, piece],
                    in0=products[(i, c0)][:, p0 : p0 + w // pieces],
                    in1=bias[:, HALF * h + piece.start : HALF * h + piece.stop],
                    op=ALU.add,
                )
            o0 = 1024 * SIG + HALF * h + c0
            nc.sync.dma_start(out=out[P * m : P * m + P, o0 : o0 + w], in_=raw[:, c0 : c0 + w])

        def displacement(i, c0=0, w=HALF, pieces=1):
            m, h = UNITS[i]
            for p0 in range(c0, c0 + w, w // pieces):
                wp = w // pieces
                s0 = STATE_COL + HALF * h + p0
                nc.vector.tensor_tensor(
                    out=plane(i, 0, p0, wp), in0=raws[i][:, p0 : p0 + wp], in1=rows_in[m][:, s0 : s0 + wp], op=ALU.subtract
                )

        def level_one(i):
            b = i % 2
            nc.vector.scalar_tensor_tensor(
                out=aux[b][:, 0, :], in0=y[b][:, 0, :], scalar=0.5, in1=aux[b][:, 2, :], op0=ALU.mult, op1=ALU.add
            )
            nc.scalar.mul(out=y[b][:, 3, :], in_=aux[b][:, 0, :], mul=tl[:, 0:1])

        def level_two(i):
            b = i % 2
            nc.vector.tensor_tensor(
                out=y[b][:, 2:5:2, :], in0=y[b][:, 0:1, :].to_broadcast([P, 2, HALF]), in1=aux[b][:, 0:2, :], op=ALU.mult
            )

        def planes_on_gpsimd(i, c0=0, w=HALF):
            b = i % 2
            cols = slice(c0, c0 + w)
            d = plane(i, 0, c0, w)
            nc.gpsimd.tensor_tensor(out=aux[b][:, 0, cols], in0=d, in1=aux[b][:, 2, cols], op=ALU.add)
            nc.scalar.mul(out=plane(i, 3, c0, w), in_=aux[b][:, 0, cols], mul=half_tl[:, 0:1])
            nc.gpsimd.tensor_tensor(out=aux[b][:, 3, cols], in0=d, in1=aux[b][:, 0, cols], op=ALU.mult)
            nc.scalar.mul(out=plane(i, 2, c0, w), in_=aux[b][:, 3, cols], mul=0.5)
            nc.gpsimd.tensor_tensor(out=plane(i, 4, c0, w), in0=d, in1=aux[b][:, 1, cols], op=ALU.mult)

        sig_banks = {}

        def copy_sigs(i, q):
            m, h = UNITS[i]
            c0 = X_COLS + SIG * (HALF * h + 128 * q)
            bank = ps_tr.tile([P, 1024], BF16, name="sp", tag="tr")
            sig_banks[(i, q)] = bank
            for a0, a1 in ((0, 512), (512, 768)):
                nc.tensor.matmul(
                    out=bank[:, a0:a1], lhsT=ident_bf[:], rhs=rows_in[m][:, c0 + a0 : c0 + a1], start=True, stop=True
                )

        out_tiles = {}

        def add_tail(i, n0, nn, engine):
            m, h = UNITS[i]
            if n0 == 256:
                new_sigs = outp.tile([P, 128, 2, SIG], F32, name="ot", align_bytes=256)
                out_tiles[i] = new_sigs
            new_sigs = out_tiles[i]
            m0 = (n0 - 256) // 2
            c0 = SIG * (HALF * h + n0)
            engine.tensor_tensor(
                out=new_sigs[:, m0 : m0 + nn // 2, :, :].rearrange("p m t c -> p m c t"),
                in0=rows_in[m][:, X_COLS + c0 : X_COLS + c0 + SIG * nn].rearrange("p (m t c) -> p m c t", t=2, c=SIG),
                in1=planes(i, n0, nn).rearrange("p c (m t) -> p m c t", t=2),
                op=ALU.add,
            )
            nc.sync.dma_start(
                out=out[P * m : P * m + P, c0 : c0 + SIG * nn],
                in_=new_sigs[:, m0 : m0 + nn // 2, :, :].rearrange("p m t c -> p (m t c)"),
            )

        def add_half(i, j):
            m, h = UNITS[i]
            new_sigs = outp.tile([P, 128, 2, SIG], F32, name="ot", align_bytes=256)
            c0 = SIG * (HALF * h + 256 * j)
            nc.vector.tensor_tensor(
                out=new_sigs[:].rearrange("p m t c -> p m c t"),
                in0=rows_in[m][:, X_COLS + c0 : X_COLS + c0 + SIG * 256].rearrange("p (m t c) -> p m c t", t=2, c=SIG),
                in1=planes(i, 256 * j, 256).rearrange("p c (m t) -> p m c t", t=2),
                op=ALU.add,
            )
            nc.sync.dma_start(
                out=out[P * m : P * m + P, c0 : c0 + SIG * 256], in_=new_sigs[:].rearrange("p m t c -> p (m t c)")
            )

        def add_quarter(i, q):
            m, h = UNITS[i]
            if q % 2 == 0:
                new_sigs = outp.tile([P, 128, 2, SIG], F32, name="ot", align_bytes=256)
                out_tiles[i] = new_sigs
            new_sigs = out_tiles[i]
            m0 = 64 * (q % 2)
            s0 = X_COLS + SIG * (HALF * h + 128 * q)
            old = sig_banks[(i, q)][:, 0:768] if (i, q) in sig_banks else rows_in[m][:, s0 : s0 + 768]
            nc.vector.tensor_tensor(
                out=new_sigs[:, m0 : m0 + 64, :, :].rearrange("p m t c -> p m c t"),
                in0=old.rearrange("p (m t c) -> p m c t", t=2, c=SIG),
                in1=planes(i, 128 * q, 128).rearrange("p c (m t) -> p m c t", t=2),
                op=ALU.add,
            )
            if i >= LAST - 2 or q % 2 == 1:
                first = q if i >= LAST - 2 else q - 1
                c0 = SIG * (HALF * h + 128 * first)
                done = new_sigs[:, 64 * (first % 2) : m0 + 64, :, :]
                nc.sync.dma_start(
                    out=out[P * m : P * m + P, c0 : c0 + SIG * 128 * (q - first + 1)],
                    in_=done.rearrange("p m t c -> p (m t c)"),
                )

        def add_and_store(i, j):
            m, h = UNITS[i]
            for n0, nn in (PARTS_OF_LAST if i == LAST else PARTS)[j]:
                new_sigs = outp.tile([P, 128, 2, SIG], F32, name="ot", align_bytes=256)
                c0 = SIG * (HALF * h + n0)
                nc.vector.tensor_tensor(
                    out=new_sigs[:, 0 : nn // 2, :, :].rearrange("p m t c -> p m c t"),
                    in0=rows_in[m][:, X_COLS + c0 : X_COLS + c0 + SIG * nn].rearrange(
                        "p (m t c) -> p m c t", t=2, c=SIG
                    ),
                    in1=y[i % 2][:, :, n0 : n0 + nn].rearrange("p c (m t) -> p m c t", t=2),
                    op=ALU.add,
                )
                nc.sync.dma_start(
                    out=out[P * m : P * m + P, c0 : c0 + SIG * nn],
                    in_=new_sigs[:, 0 : nn // 2, :, :].rearrange("p m t c -> p (m t c)"),
                )

        nc.scalar.activation(out=warm[:], in_=warm[:], func=ACT.Exp)
        for k in range(len(CHUNKS)):
            transpose_chunk(0, k)
            quantise_chunk(0, k)
        spread = ps_acc.tile([P, HALF], F32, name="acc")
        nc.tensor.matmul(out=spread[:, 0:2], lhsT=ones[:], rhs=log_row[:], start=True, stop=True)
        nc.scalar.activation(out=tl[:], in_=spread[:, 0:1], func=ACT.Exp)
        nc.vector.tensor_scalar_mul(out=half_tl[:], in0=tl[:], scalar1=0.5)
        for b in range(2):
            nc.vector.tensor_copy(out=y[b][:, 1, :], in_=tl[:, 0:1].to_broadcast([P, HALF]))
        for h in range(2):
            spread = ps_acc.tile([P, HALF], F32, name="acc")
            nc.tensor.matmul(
                out=spread[:], lhsT=ones[:], rhs=bias_rows[:, HALF * h : HALF * (h + 1)], start=True, stop=True
            )
            nc.scalar.copy(out=bias[:, HALF * h : HALF * (h + 1)], in_=spread[:])
        for k in range(len(CHUNKS)):
            transpose_chunk(1, k)
            quantise_chunk(1, k)
        if 0 in FED:
            for q in range(4):
                copy_sigs(0, q)
        from_inputs(0)
        product(0)
        product(1)
        add_bias(0, pieces=2)
        displacement(0, pieces=2)
        level_one(0)
        level_two(0)

        TILE_IN = {1: 2, 2: 3}
        for i in range(len(UNITS)):
            nxt = i + 1
            new_tile = TILE_IN.get(i)
            if nxt <= LAST:
                from_inputs(nxt)
            if new_tile:
                transpose_chunk(new_tile, 0)
                transpose_chunk(new_tile, 1)
            if i + 2 < LAST:
                product(i + 2)
            if i + 2 == LAST:
                narrow_product(LAST, 0)
            if new_tile:
                for k in range(2, len(CHUNKS)):
                    transpose_chunk(new_tile, k)
            if nxt == LAST:
                for c0 in (0, 256):
                    add_bias(nxt, c0, 256)
                    add_quarter(i, c0 // 128)
                    displacement(nxt, c0, 256)
                    planes_on_gpsimd(nxt, c0, 256)
                    add_quarter(i, c0 // 128 + 1)
                    if c0 == 0:
                        for q in range(2):
                            copy_sigs(nxt, q)
            elif nxt in ON_GPSIMD:
                add_bias(nxt, pieces=2)
                displacement(nxt, pieces=2)
                planes_on_gpsimd(nxt)
                for q in range(4):
                    add_quarter(i, q)
                    if nxt in FED:
                        copy_sigs(nxt, q)
                    if i + 2 == LAST and q == 1:
                        narrow_product(LAST, 256)
            elif nxt < LAST:
                add_bias(nxt)
                add_half(i, 0)
                displacement(nxt)
                add_half(i, 1)
                level_one(nxt)
                quantise_chunk(new_tile, 0)
                level_two(nxt)
                if nxt in FED:
                    for q in range(4):
                        copy_sigs(nxt, q)
            else:
                add_quarter(i, 0)
                add_quarter(i, 1)
                for n0, nn in ((256, 128), (384, 64), (448, 64)):
                    add_tail(i, n0, nn, nc.vector)
            if new_tile:
                for k in range(1, len(CHUNKS)):
                    quantise_chunk(new_tile, k)
            if i == 0:
                load_rows(3)
